import numpy as np
import ml_dtypes


def mxq(x, axis, fmt="e4m3"):
    dtype, down = {"e4m3": (ml_dtypes.float8_e4m3fn, 7), "e5m2": (ml_dtypes.float8_e5m2, 14)}[fmt]
    v = np.moveaxis(np.asarray(x, np.float32).astype(ml_dtypes.bfloat16).astype(np.float64), axis, -1)
    blocks = v.reshape(v.shape[:-1] + (-1, 32))
    amax = np.abs(blocks).max(-1, keepdims=True)
    byte = np.maximum(np.where(amax > 0, np.frexp(amax)[1] - 1 + 127, 0) - down, 1)
    scale = np.exp2(byte - 127.0)
    codes = (blocks / scale).astype(np.float32).astype(dtype).astype(np.float64)
    return np.moveaxis((codes * scale).reshape(v.shape), -1, axis)


WIDE = False


def mx_kscale(k):
    if not WIDE:
        return np.ones(k)
    levels = np.array([10, -10, 5, -5, 0])
    a = np.random.permutation(np.resize(levels, k // 512 * 4)).reshape(k // 512, 4)
    idx = np.arange(k)
    return np.exp2(a[idx // 512, idx % 128 // 32])


BF16 = ml_dtypes.bfloat16


def bf(x):
    return np.asarray(x, np.float32).astype(BF16)


def f64(x):
    return np.asarray(x).astype(np.float64)


B, SA, SB, D, H, DH = 1, 768, 256, 1024, 8, 128
S = SA + SB
EPS = 1e-6


def make_rope(s, dh):
    pos = np.arange(s, dtype=np.float64)
    inv_freq = 1.0 / (10000.0 ** (np.arange(0, dh, 2, dtype=np.float64) / dh))
    theta = pos[:, None] * inv_freq[None, :]
    cos, sin = np.cos(theta), np.sin(theta)
    row0 = np.stack([cos, -sin], axis=-1)
    row1 = np.stack([sin, cos], axis=-1)
    return np.stack([row0, row1], axis=-2)[None, None]


def rms_norm(x, w):
    return x * (1.0 / np.sqrt(np.mean(x * x, axis=-1, keepdims=True) + EPS)) * w


def apply_rope(x, freqs):
    x_ = x.reshape(*x.shape[:-1], -1, 1, 2)
    out = freqs[..., 0] * x_[..., 0] + freqs[..., 1] * x_[..., 1]
    return out.reshape(x.shape)


def qkv(x, w, b):
    y = (mxq(x, 2, "e4m3") @ mxq(w, 1, "e4m3").T) + b
    y = y.reshape(x.shape[0], x.shape[1], 3 * H, DH).transpose(0, 2, 1, 3)
    return y[:, :H], y[:, H:2 * H], y[:, 2 * H:]


def setup_inputs():
    sa, sb = mx_kscale(D), mx_kscale(D)
    return {
        "hidden_states_a": bf(np.random.standard_normal((B, SA, D)) * sa),
        "hidden_states_b": bf(np.random.standard_normal((B, SB, D)) * sb),
        "image_rotary_emb": bf(make_rope(S, DH)),
        "a_qkv_w": bf(np.random.standard_normal((3 * D, D)) / np.sqrt(D) / sa),
        "a_qkv_b": bf(np.random.standard_normal(3 * D) * 0.2),
        "b_qkv_w": bf(np.random.standard_normal((3 * D, D)) / np.sqrt(D) / sb),
        "b_qkv_b": bf(np.random.standard_normal(3 * D) * 0.2),
        "norm_q_a_w": bf(1.5 + 0.15 * np.random.standard_normal(DH)),
        "norm_k_a_w": bf(1.5 + 0.15 * np.random.standard_normal(DH)),
        "norm_q_b_w": bf(1.5 + 0.15 * np.random.standard_normal(DH)),
        "norm_k_b_w": bf(1.5 + 0.15 * np.random.standard_normal(DH)),
    }


def reference(hidden_states_a, hidden_states_b, image_rotary_emb, a_qkv_w, a_qkv_b, b_qkv_w, b_qkv_b,
              norm_q_a_w, norm_k_a_w, norm_q_b_w, norm_k_b_w):
    q_a, k_a, v_a = qkv(f64(hidden_states_a), f64(a_qkv_w), f64(a_qkv_b))
    q_a = rms_norm(q_a, f64(norm_q_a_w))
    k_a = rms_norm(k_a, f64(norm_k_a_w))
    q_b, k_b, v_b = qkv(f64(hidden_states_b), f64(b_qkv_w), f64(b_qkv_b))
    q_b = rms_norm(q_b, f64(norm_q_b_w))
    k_b = rms_norm(k_b, f64(norm_k_b_w))
    q = np.concatenate([q_b, q_a], axis=2)
    k = np.concatenate([k_b, k_a], axis=2)
    v = np.concatenate([v_b, v_a], axis=2)
    f = f64(image_rotary_emb)
    return apply_rope(q, f), apply_rope(k, f), v

@@ -1,0 +1,384 @@
+from contextlib import ExitStack
+
+import concourse.mybir as mybir
+from concourse.masks import make_identity
+
+FLOPS = 2 * 1024 * 1024 * 3072
+
+F32 = mybir.dt.float32
+BF16 = mybir.dt.bfloat16
+U32 = mybir.dt.uint32
+U8 = mybir.dt.uint8
+FP8X4 = mybir.dt.float8_e4m3fn_x4
+ACT = mybir.ActivationFunctionType
+ALU = mybir.AluOpType
+
+P = 128
+K = 1024
+NQK = 16
+EPS = 1e-6
+PIN = True
+V_EXIT_EVERY = 2
+
+
+def x_word(blk, g):
+    if blk < 4:
+        return g * 512 + blk * 128
+    if blk < 6:
+        return 1024 + g * 256 + (blk - 4) * 128
+    return 1536 + g * 256 + (blk - 6) * 128
+
+
+def tile_fluxjointattention_pa_kernel(
+    tc,
+    hidden_states_a,
+    hidden_states_b,
+    image_rotary_emb,
+    a_qkv_w,
+    a_qkv_b,
+    b_qkv_w,
+    b_qkv_b,
+    norm_q_a_w,
+    norm_k_a_w,
+    norm_q_b_w,
+    norm_k_b_w,
+    out_0,
+    out_1,
+    out_2,
+):
+    nc = tc.nc
+    with ExitStack() as ctx:
+        if PIN:
+            ctx.enter_context(tc.manual_schedule())
+        const = ctx.enter_context(tc.tile_pool(name="const", bufs=1))
+        raws = ctx.enter_context(tc.tile_pool(name="raws", bufs=6))
+        grps = ctx.enter_context(tc.tile_pool(name="grps", bufs=2))
+        cods = ctx.enter_context(tc.tile_pool(name="cods", bufs=4))
+        work = ctx.enter_context(tc.tile_pool(name="work", bufs=4))
+        outs = ctx.enter_context(tc.tile_pool(name="outs", bufs=2))
+        ps_prep = ctx.enter_context(tc.psum_pool(name="psprep", bufs=2))
+        ps_acc = ctx.enter_context(tc.psum_pool(name="psacc", bufs=2))
+        ps_y = ctx.enter_context(tc.psum_pool(name="psy", bufs=4))
+
+        xa_v = hidden_states_a.rearrange("o (p t) k -> p (o t) k", t=6)
+        xb_v = hidden_states_b.rearrange("o (p t) k -> p (o t) k", t=2)
+        w_v = [
+            a_qkv_w.rearrange("(n p) k -> p n k", p=P),
+            b_qkv_w.rearrange("(n p) k -> p n k", p=P),
+        ]
+        rope_v = image_rotary_emb.rearrange("a b s j i c -> (a b s) (j i c)")
+        biases = [a_qkv_b, b_qkv_b]
+        gains = [norm_q_a_w, norm_k_a_w, norm_q_b_w, norm_k_b_w]
+        qk_out = [out_0, out_1]
+
+        eps_t = const.tile([P, 1], F32, name="eps_t")
+        nc.vector.memset(eps_t[:], EPS)
+        warm = const.tile([P, 1], F32, name="warm")
+        nc.scalar.activation(out=warm[:], in_=eps_t[:], func=ACT.Sqrt)
+        brow = const.tile([P, P], BF16, name="brow")
+        nc.vector.memset(brow[:], 0.0)
+        ident = const.tile([P, P], F32, name="ident")
+        make_identity(nc, ident[:])
+
+        raw_x0 = raws.tile([P, 4, K], BF16, name="raw_x0", tag="raw")
+        nc.sync.dma_start(out=raw_x0[:], in_=xa_v[:, 0:4, :])
+        raw_x1 = raws.tile([P, 4, K], BF16, name="raw_x1", tag="raw")
+        nc.sync.dma_start(out=raw_x1[:, 0:2, :], in_=xa_v[:, 4:6, :])
+        nc.sync.dma_start(out=raw_x1[:, 2:4, :], in_=xb_v)
+
+        vbias = const.tile([P, 2, 1024], BF16, name="vbias")
+        nc.gpsimd.dma_start(out=vbias[:, 0, :], in_=biases[0][2048:3072].partition_broadcast(P))
+        for s in range(2):
+            nc.gpsimd.dma_start(
+                out=brow[16 * s : 16 * s + 16, :],
+                in_=biases[s][0:2048].rearrange("(r f) -> r f", f=P),
+            )
+        rope = const.tile([P, 8, 256], BF16, name="rope")
+        nc.gpsimd.dma_start(out=rope[:, 0:6, :], in_=rope_v[256:1024, :].rearrange("(p t) e -> p t e", t=6))
+        nc.gpsimd.dma_start(out=rope[:, 6:8, :], in_=rope_v[0:256, :].rearrange("(p t) e -> p t e", t=2))
+        gain = const.tile([P, 4, P], BF16, name="gain")
+        for m in range(4):
+            nc.gpsimd.dma_start(out=gain[:, m, :], in_=gains[m].partition_broadcast(P))
+        nc.gpsimd.dma_start(out=vbias[:, 1, :], in_=biases[1][2048:3072].partition_broadcast(P))
+
+        raw_w = {}
+
+        def load_w(s, chunk):
+            t = raws.tile([P, 4, K], BF16, name="raw_w%d_%d" % (s, chunk), tag="raw")
+            nc.sync.dma_start(out=t[:], in_=w_v[s][:, 4 * chunk : 4 * chunk + 4, :])
+            raw_w[(s, chunk)] = t
+
+        def prep(raw2d, dst, pool, tag, on_vector):
+            bank = pool.tile([P, 512], F32, name="bank_" + tag, tag=tag)
+            words = raw2d.bitcast(F32)
+            for gu in range(4):
+                nc.tensor.transpose(bank[:, gu * P : (gu + 1) * P], words[:, gu * P : (gu + 1) * P], ident[:])
+            src = bank[:].rearrange("p (g u n) -> p g n u", g=2, u=2)
+            if on_vector:
+                nc.vector.tensor_copy(out=dst, in_=src)
+            else:
+                nc.scalar.copy(out=dst, in_=src)
+
+        load_w(0, 4)
+        load_w(0, 5)
+
+        x_codes = const.tile([P, 2048], U32, name="x_codes", align_bytes=64)
+        x_scale = const.tile([P, 2048], U8, name="x_scale", align_bytes=64)
+        xg0 = grps.tile([P, 4096], BF16, name="xg0", tag="grp8", align_bytes=64)
+        xg1 = grps.tile([P, 4096], BF16, name="xg1", tag="grp8", align_bytes=64)
+        xg0_v = xg0[:].bitcast(F32).rearrange("p (g n u) -> p g n u", g=2, u=2)
+        xg1_v = xg1[:].bitcast(F32).rearrange("p (c g n u) -> p c g n u", c=2, g=2, u=2)
+
+        def quant(codes, scales, grp, w0, w1, g0):
+            nc.vector.quantize_mx(
+                out=codes[:, w0:w1].bitcast(FP8X4),
+                scales=scales[:, w0:w1],
+                in_=grp[:, g0 : g0 + 4 * (w1 - w0)],
+            )
+
+        for blk in range(8):
+            pool, tag = [(ps_prep, "prep"), (ps_acc, "acc")][(blk // 2) % 2]
+            if blk < 4:
+                prep(raw_x0[:, blk, :], xg0_v[:, :, blk * P : (blk + 1) * P, :], pool, tag, blk % 2 == 1)
+            else:
+                c, tb = divmod(blk - 4, 2)
+                prep(raw_x1[:, blk - 4, :], xg1_v[:, c, :, tb * P : (tb + 1) * P, :], pool, tag, blk % 2 == 1)
+            if blk == 3:
+                quant(x_codes, x_scale, xg0, 0, 1024, 0)
+            if blk == 5:
+                quant(x_codes, x_scale, xg1, 1024, 1536, 0)
+            if blk == 7:
+                quant(x_codes, x_scale, xg1, 1536, 2048, 2048)
+
+        load_w(0, 0)
+        load_w(1, 0)
+        load_w(0, 1)
+        load_w(1, 1)
+
+        brow_f = const.tile([P, P], F32, name="brow_f")
+        nc.vector.tensor_copy(out=brow_f[:], in_=brow[:])
+        bias_ps = ps_prep.tile([P, 512], F32, name="bias_ps", tag="prep")
+        nc.tensor.transpose(bias_ps[:, 0:P], brow_f[:], ident[:])
+        bias_t = const.tile([P, 32], F32, name="bias_t")
+        nc.vector.tensor_copy(out=bias_t[:], in_=bias_ps[:, 0:32])
+
+        gain_x = const.tile([P, 4, 2, 64], BF16, name="gain_x")
+        gain_p = gain[:].rearrange("p m (j c) -> p m j c", c=2)
+        for i in range(2):
+            nc.gpsimd.tensor_copy(out=gain_x[:, :, i, :], in_=gain_p[:, :, :, 1 - i])
+        tab_a = [const.tile([P, 8, P], F32, name="tab_a%d" % kind) for kind in range(2)]
+        tab_b = [const.tile([P, 8, 2, 64], F32, name="tab_b%d" % kind) for kind in range(2)]
+        rope_q = rope[:].rearrange("p t (j q) -> p t j q", q=4)
+        for kind in range(2):
+            for s, b0, b1 in ((0, 0, 6), (1, 6, 8)):
+                m = 2 * s + kind
+                nb = b1 - b0
+                nc.gpsimd.tensor_tensor(
+                    out=tab_a[kind][:, b0:b1, :].rearrange("p t (j c) -> p t j c", c=2),
+                    in0=rope_q[:, b0:b1, :, 0:4:3],
+                    in1=gain_p[:, m, :, :].unsqueeze(1).to_broadcast([P, nb, 64, 2]),
+                    op=ALU.mult,
+                )
+                nc.gpsimd.tensor_tensor(
+                    out=tab_b[kind][:, b0:b1, :, :],
+                    in0=rope_q[:, b0:b1, :, 1:3].rearrange("p t j c -> p t c j"),
+                    in1=gain_x[:, m, :, :].unsqueeze(1).to_broadcast([P, nb, 2, 64]),
+                    op=ALU.mult,
+                )
+
+        v_codes = {}
+
+        def v_prep(s, c):
+            vg = grps.tile([P, 4096], BF16, name="vg", tag="grp8", align_bytes=64)
+            vg_v = vg[:].bitcast(F32).rearrange("p (g n u) -> p g n u", g=2, u=2)
+            raw = raw_w[(s, 4 + c)]
+            for j in range(4):
+                pool, tag = [(ps_prep, "prep"), (ps_acc, "acc")][(j // 2) % 2]
+                prep(raw[:, j, :], vg_v[:, :, j * P : (j + 1) * P, :], pool, tag, False)
+            vc = const.tile([P, 1024], U32, name="vc%d%d" % (s, c), align_bytes=64)
+            vs = const.tile([P, 1024], U8, name="vs%d%d" % (s, c), align_bytes=64)
+            quant(vc, vs, vg, 0, 1024, 0)
+            v_codes[(s, c)] = (vc, vs)
+
+        def v_mult(s, c):
+            vc, vs = v_codes[(s, c)]
+            b0, nt = ((0, 6), (6, 2))[s]
+            ov = outs.tile([P, 4, nt, P], F32, name="ov%d" % s)
+            for t in range(nt):
+                acc = ps_y.tile([P, 512], F32, name="vacc", tag="y")
+                for g in range(2):
+                    xo = x_word(b0 + t, g)
+                    nc.tensor.matmul_mx(
+                        out=acc[:],
+                        lhsT=x_codes[:, xo : xo + P].bitcast(FP8X4),
+                        lhsT_scale=x_scale[:, xo : xo + P],
+                        rhs=vc[:, g * 512 : (g + 1) * 512].bitcast(FP8X4),
+                        rhs_scale=vs[:, g * 512 : (g + 1) * 512],
+                        start=(g == 0),
+                        stop=(g == 1),
+                    )
+                nc.vector.tensor_tensor(
+                    out=ov[:, :, t, :],
+                    in0=acc[:].rearrange("p (h f) -> p h f", h=4),
+                    in1=vbias[:, s, c * 512 : (c + 1) * 512].rearrange("p (h f) -> p h f", h=4),
+                    op=ALU.add,
+                )
+            lo, hi = ((256, 1024), (0, 256))[s]
+            nc.sync.dma_start(
+                out=out_2[0, 4 * c : 4 * c + 4, lo:hi, :].rearrange("h (p t) f -> p h (t f)", t=nt),
+                in_=ov[:].rearrange("p h t f -> p h (t f)"),
+            )
+
+        st = {}
+
+        def qk_prep(h):
+            grp = grps.tile([P, 2048], BF16, name="grp", tag="grp4", align_bytes=64)
+            grp_v = grp[:].bitcast(F32).rearrange("p (s g n u) -> p s g n u", s=2, g=2, u=2)
+            banks = []
+            for s in range(2):
+                bank = ps_prep.tile([P, 512], F32, name="bank_qk", tag="prep")
+                words = raw_w[(s, h // 4)][:, h % 4, :].bitcast(F32)
+                for gu in range(4):
+                    nc.tensor.transpose(bank[:, gu * P : (gu + 1) * P], words[:, gu * P : (gu + 1) * P], ident[:])
+                banks.append(bank)
+            st[("prep", h)] = (grp, grp_v, banks)
+
+        def qk_exit(h):
+            grp, grp_v, banks = st[("prep", h)]
+            for s in range(2):
+                src = banks[s][:].rearrange("p (g u n) -> p g n u", g=2, u=2)
+                if s == 1 and h % V_EXIT_EVERY == 0:
+                    nc.vector.tensor_copy(out=grp_v[:, s, :, :, :], in_=src)
+                else:
+                    nc.scalar.copy(out=grp_v[:, s, :, :, :], in_=src)
+
+        def qk_quant(h):
+            grp, grp_v, banks = st[("prep", h)]
+            wc = cods.tile([P, 512], U32, name="wc", align_bytes=64)
+            ws = cods.tile([P, 512], U8, name="ws", align_bytes=64)
+            quant(wc, ws, grp, 0, 512, 0)
+            st[("codes", h)] = (wc, ws)
+
+        def qk_mult(h):
+            wc, ws = st[("codes", h)]
+            accs = [ps_acc.tile([P, 512], F32, name="acc", tag="acc") for b in range(2)]
+            for bank, c0, n, s, xw in ((0, 0, 512, 0, 0), (1, 0, 256, 0, 1024), (1, 256, 256, 1, 1536)):
+                for g in range(2):
+                    wo = (2 * s + g) * P
+                    xo = xw + g * n
+                    nc.tensor.matmul_mx(
+                        out=accs[bank][:, c0 : c0 + n],
+                        lhsT=wc[:, wo : wo + P].bitcast(FP8X4),
+                        lhsT_scale=ws[:, wo : wo + P],
+                        rhs=x_codes[:, xo : xo + n].bitcast(FP8X4),
+                        rhs_scale=x_scale[:, xo : xo + n],
+                        start=(g == 0),
+                        stop=(g == 1),
+                    )
+            st[("acc", h)] = accs
+
+        def qk_bias(h):
+            accs = st[("acc", h)]
+            yts = [work.tile([P, 512], F32, name="yt") for b in range(2)]
+            for bank, c0, n, s in ((0, 0, 512, 0), (1, 0, 256, 0), (1, 256, 256, 1)):
+                nc.scalar.activation(
+                    out=yts[bank][:, c0 : c0 + n],
+                    in_=accs[bank][:, c0 : c0 + n],
+                    func=ACT.Identity,
+                    bias=bias_t[:, 16 * s + h : 16 * s + h + 1],
+                    scale=1.0,
+                )
+            st[("yt", h)] = yts
+
+        def qk_back(h):
+            yts = st[("yt", h)]
+            ys = []
+            for bank in range(2):
+                y = ps_y.tile([P, 512], F32, name="y", tag="y")
+                for b in range(4):
+                    nc.tensor.transpose(y[:, b * P : (b + 1) * P], yts[bank][:, b * P : (b + 1) * P], ident[:])
+                ys.append(y)
+            st[("y", h)] = ys
+
+        junk = const.tile([P, P], F32, name="junk")
+
+        def qk_tail(h):
+            ys = st[("y", h)]
+            kind = h // 8
+            o = outs.tile([P, 8, P], F32, name="o", bufs=3)
+            for bank in range(2):
+                y = ys[bank]
+                ss = work.tile([P, 4], F32, name="ss")
+                sd = work.tile([P, 4], F32, name="sd")
+                rs = work.tile([P, 4], F32, name="rs")
+                for b in range(4):
+                    nc.scalar.activation(
+                        out=junk[:], in_=y[:, b * P : (b + 1) * P], func=ACT.Square, accum_out=ss[:, b : b + 1]
+                    )
+                nc.scalar.activation(out=sd[:], in_=ss[:], func=ACT.Sqrt, bias=eps_t[:], scale=1.0 / P)
+                nc.vector.reciprocal(out=rs[:], in_=sd[:])
+                m1 = work.tile([P, 4, P], F32, name="m1")
+                m2 = work.tile([P, 4, 2, 64], F32, name="m2")
+                for b in range(4):
+                    blk = 4 * bank + b
+                    yb = y[:, b * P : (b + 1) * P]
+                    nc.vector.scalar_tensor_tensor(
+                        out=m1[:, b, :], in0=yb, scalar=rs[:, b : b + 1], in1=tab_a[kind][:, blk, :],
+                        op0=ALU.mult, op1=ALU.mult,
+                    )
+                    yp = yb.rearrange("p (j c) -> p j c", c=2)
+                    for i in range(2):
+                        nc.vector.scalar_tensor_tensor(
+                            out=m2[:, b, i, :], in0=yp[:, :, 1 - i], scalar=rs[:, b : b + 1],
+                            in1=tab_b[kind][:, blk, i, :], op0=ALU.mult, op1=ALU.mult,
+                        )
+                nc.gpsimd.tensor_tensor(
+                    out=o[:, 4 * bank : 4 * bank + 4, :].rearrange("p b (j c) -> p b j c", c=2),
+                    in0=m1[:].rearrange("p b (j c) -> p b j c", c=2),
+                    in1=m2[:].rearrange("p b c j -> p b j c"),
+                    op=ALU.add,
+                )
+            dst = qk_out[kind]
+            nc.sync.dma_start(
+                out=dst[0, h % 8, 256:1024, :].rearrange("(p t) f -> p (t f)", t=6),
+                in_=o[:, 0:6, :].rearrange("p t f -> p (t f)"),
+            )
+            nc.sync.dma_start(
+                out=dst[0, h % 8, 0:256, :].rearrange("(p t) f -> p (t f)", t=2),
+                in_=o[:, 6:8, :].rearrange("p t f -> p (t f)"),
+            )
+
+        v_prep(0, 0)
+        load_w(0, 2)
+        v_prep(0, 1)
+        load_w(1, 2)
+        v_mult(0, 0)
+        for h in range(2):
+            qk_prep(h)
+            qk_exit(h)
+            qk_quant(h)
+        v_mult(0, 1)
+        for h in range(NQK + 1):
+            if h >= 1:
+                qk_back(h - 1)
+            if h + 2 < NQK:
+                qk_prep(h + 2)
+            if h < NQK:
+                qk_mult(h)
+            if h >= 1:
+                qk_tail(h - 1)
+            if h < NQK:
+                qk_bias(h)
+            if h + 2 < NQK:
+                qk_exit(h + 2)
+                qk_quant(h + 2)
+            if h == 1:
+                load_w(0, 3)
+                load_w(1, 3)
+            if h == 5:
+                load_w(1, 4)
+                load_w(1, 5)
+        v_prep(1, 0)
+        v_prep(1, 1)
+        v_mult(1, 0)
+        v_mult(1, 1)

@@ -18,7 +18,8 @@ K = 1024
 NQK = 16
 EPS = 1e-6
 PIN = True
-V_EXIT_EVERY = 2
+V_EXITS = (0, 2, 4, 6, 8, 10, 12)
+FILL = 2
 
 
 def x_word(blk, g):
@@ -51,7 +52,7 @@ def tile_fluxjointattention_pa_kernel(
         if PIN:
             ctx.enter_context(tc.manual_schedule())
         const = ctx.enter_context(tc.tile_pool(name="const", bufs=1))
-        raws = ctx.enter_context(tc.tile_pool(name="raws", bufs=6))
+        raws = ctx.enter_context(tc.tile_pool(name="raws", bufs=4))
         grps = ctx.enter_context(tc.tile_pool(name="grps", bufs=2))
         cods = ctx.enter_context(tc.tile_pool(name="cods", bufs=4))
         work = ctx.enter_context(tc.tile_pool(name="work", bufs=4))
@@ -80,54 +81,34 @@ def tile_fluxjointattention_pa_kernel(
         ident = const.tile([P, P], F32, name="ident")
         make_identity(nc, ident[:])
 
-        raw_x0 = raws.tile([P, 4, K], BF16, name="raw_x0", tag="raw")
-        nc.sync.dma_start(out=raw_x0[:], in_=xa_v[:, 0:4, :])
-        raw_x1 = raws.tile([P, 4, K], BF16, name="raw_x1", tag="raw")
-        nc.sync.dma_start(out=raw_x1[:, 0:2, :], in_=xa_v[:, 4:6, :])
-        nc.sync.dma_start(out=raw_x1[:, 2:4, :], in_=xb_v)
-
         vbias = const.tile([P, 2, 1024], BF16, name="vbias")
+        rope = const.tile([P, 8, 256], BF16, name="rope")
+        gain = const.tile([P, 4, P], BF16, name="gain")
         nc.gpsimd.dma_start(out=vbias[:, 0, :], in_=biases[0][2048:3072].partition_broadcast(P))
+        nc.gpsimd.dma_start(out=rope[:, 0:6, :], in_=rope_v[256:1024, :].rearrange("(p t) e -> p t e", t=6))
+        nc.gpsimd.dma_start(out=rope[:, 6:8, :], in_=rope_v[0:256, :].rearrange("(p t) e -> p t e", t=2))
+        for m in (0, 2, 1, 3):
+            nc.gpsimd.dma_start(out=gain[:, m, :], in_=gains[m].partition_broadcast(P))
         for s in range(2):
             nc.gpsimd.dma_start(
                 out=brow[16 * s : 16 * s + 16, :],
                 in_=biases[s][0:2048].rearrange("(r f) -> r f", f=P),
             )
-        rope = const.tile([P, 8, 256], BF16, name="rope")
-        nc.gpsimd.dma_start(out=rope[:, 0:6, :], in_=rope_v[256:1024, :].rearrange("(p t) e -> p t e", t=6))
-        nc.gpsimd.dma_start(out=rope[:, 6:8, :], in_=rope_v[0:256, :].rearrange("(p t) e -> p t e", t=2))
-        gain = const.tile([P, 4, P], BF16, name="gain")
-        for m in range(4):
-            nc.gpsimd.dma_start(out=gain[:, m, :], in_=gains[m].partition_broadcast(P))
         nc.gpsimd.dma_start(out=vbias[:, 1, :], in_=biases[1][2048:3072].partition_broadcast(P))
 
         raw_w = {}
 
-        def load_w(s, chunk):
-            t = raws.tile([P, 4, K], BF16, name="raw_w%d_%d" % (s, chunk), tag="raw")
-            nc.sync.dma_start(out=t[:], in_=w_v[s][:, 4 * chunk : 4 * chunk + 4, :])
-            raw_w[(s, chunk)] = t
+        def load_w(s, chunk, j0, j1):
+            if j0 == 0:
+                raw_w[(s, chunk)] = raws.tile([P, 4, K], BF16, name="raw_w%d_%d" % (s, chunk), tag="raw")
+            nc.sync.dma_start(out=raw_w[(s, chunk)][:, j0:j1, :], in_=w_v[s][:, 4 * chunk + j0 : 4 * chunk + j1, :])
 
-        def prep(raw2d, dst, pool, tag, on_vector):
-            bank = pool.tile([P, 512], F32, name="bank_" + tag, tag=tag)
-            words = raw2d.bitcast(F32)
-            for gu in range(4):
-                nc.tensor.transpose(bank[:, gu * P : (gu + 1) * P], words[:, gu * P : (gu + 1) * P], ident[:])
-            src = bank[:].rearrange("p (g u n) -> p g n u", g=2, u=2)
-            if on_vector:
-                nc.vector.tensor_copy(out=dst, in_=src)
-            else:
-                nc.scalar.copy(out=dst, in_=src)
-
-        load_w(0, 4)
-        load_w(0, 5)
-
-        x_codes = const.tile([P, 2048], U32, name="x_codes", align_bytes=64)
-        x_scale = const.tile([P, 2048], U8, name="x_scale", align_bytes=64)
-        xg0 = grps.tile([P, 4096], BF16, name="xg0", tag="grp8", align_bytes=64)
-        xg1 = grps.tile([P, 4096], BF16, name="xg1", tag="grp8", align_bytes=64)
-        xg0_v = xg0[:].bitcast(F32).rearrange("p (g n u) -> p g n u", g=2, u=2)
-        xg1_v = xg1[:].bitcast(F32).rearrange("p (c g n u) -> p c g n u", c=2, g=2, u=2)
+        def load_v(s, c, j0, j1):
+            if j0 == 0:
+                raw_w[(s, 4 + c)] = raws.tile([P, 4, K], BF16, name="raw_v%d_%d" % (s, c), tag="rawv", bufs=2)
+            nc.sync.dma_start(
+                out=raw_w[(s, 4 + c)][:, j0:j1, :], in_=w_v[s][:, 16 + 4 * c + j0 : 16 + 4 * c + j1, :]
+            )
 
         def quant(codes, scales, grp, w0, w1, g0):
             nc.vector.quantize_mx(
@@ -136,138 +117,181 @@ def tile_fluxjointattention_pa_kernel(
                 in_=grp[:, g0 : g0 + 4 * (w1 - w0)],
             )
 
-        for blk in range(8):
-            pool, tag = [(ps_prep, "prep"), (ps_acc, "acc")][(blk // 2) % 2]
+        raw_x = [raws.tile([P, 4, K], BF16, name="raw_x%d" % i, tag="raw") for i in range(2)]
+        x_codes = const.tile([P, 2048], U32, name="x_codes", align_bytes=64)
+        x_scale = const.tile([P, 2048], U8, name="x_scale", align_bytes=64)
+        xg = [grps.tile([P, 4096], BF16, name="xg%d" % i, tag="grp8", align_bytes=64) for i in range(2)]
+        xg0_v = xg[0][:].bitcast(F32).rearrange("p (g n u) -> p g n u", g=2, u=2)
+        xg1_v = xg[1][:].bitcast(F32).rearrange("p (c g n u) -> p c g n u", c=2, g=2, u=2)
+        x_bank = {}
+
+        def load_x(pair):
+            src = (xa_v[:, 0:2, :], xa_v[:, 2:4, :], xa_v[:, 4:6, :], xb_v)[pair]
+            nc.sync.dma_start(out=raw_x[pair // 2][:, 2 * (pair % 2) : 2 * (pair % 2) + 2, :], in_=src)
+
+        def x_tr(blk):
+            pool, tag = ((ps_prep, "prep"), (ps_acc, "acc"), (ps_y, "y"), (ps_y, "y"))[blk // 2]
+            bank = pool.tile([P, 512], F32, name="bank_x", tag=tag)
+            words = raw_x[blk // 4][:, blk % 4, :].bitcast(F32)
+            for gu in range(4):
+                nc.tensor.transpose(bank[:, gu * P : (gu + 1) * P], words[:, gu * P : (gu + 1) * P], ident[:])
+            x_bank[blk] = bank
+
+        def x_exit(blk, on_vector):
             if blk < 4:
-                prep(raw_x0[:, blk, :], xg0_v[:, :, blk * P : (blk + 1) * P, :], pool, tag, blk % 2 == 1)
+                dst = xg0_v[:, :, blk * P : (blk + 1) * P, :]
             else:
                 c, tb = divmod(blk - 4, 2)
-                prep(raw_x1[:, blk - 4, :], xg1_v[:, c, :, tb * P : (tb + 1) * P, :], pool, tag, blk % 2 == 1)
-            if blk == 3:
-                quant(x_codes, x_scale, xg0, 0, 1024, 0)
-            if blk == 5:
-                quant(x_codes, x_scale, xg1, 1024, 1536, 0)
-            if blk == 7:
-                quant(x_codes, x_scale, xg1, 1536, 2048, 2048)
+                dst = xg1_v[:, c, :, tb * P : (tb + 1) * P, :]
+            src = x_bank[blk][:].rearrange("p (g u n) -> p g n u", g=2, u=2)
+            if on_vector:
+                nc.vector.tensor_copy(out=dst, in_=src)
+            else:
+                nc.scalar.copy(out=dst, in_=src)
 
-        load_w(0, 0)
-        load_w(1, 0)
-        load_w(0, 1)
-        load_w(1, 1)
+        def x_quant(c):
+            if c == 0:
+                quant(x_codes, x_scale, xg[0], 0, 1024, 0)
+            else:
+                quant(x_codes, x_scale, xg[1], 512 + 512 * c, 1024 + 512 * c, 2048 * (c - 1))
 
-        brow_f = const.tile([P, P], F32, name="brow_f")
-        nc.vector.tensor_copy(out=brow_f[:], in_=brow[:])
-        bias_ps = ps_prep.tile([P, 512], F32, name="bias_ps", tag="prep")
-        nc.tensor.transpose(bias_ps[:, 0:P], brow_f[:], ident[:])
         bias_t = const.tile([P, 32], F32, name="bias_t")
-        nc.vector.tensor_copy(out=bias_t[:], in_=bias_ps[:, 0:32])
 
-        gain_x = const.tile([P, 4, 2, 64], BF16, name="gain_x")
+        def bias_columns():
+            brow_f = const.tile([P, P], F32, name="brow_f")
+            nc.vector.tensor_copy(out=brow_f[:], in_=brow[:])
+            bias_ps = ps_prep.tile([P, 512], F32, name="bias_ps", tag="prep")
+            nc.tensor.transpose(bias_ps[:, 0:P], brow_f[:], ident[:])
+            nc.vector.tensor_copy(out=bias_t[:], in_=bias_ps[:, 0:32])
+
         gain_p = gain[:].rearrange("p m (j c) -> p m j c", c=2)
-        for i in range(2):
-            nc.gpsimd.tensor_copy(out=gain_x[:, :, i, :], in_=gain_p[:, :, :, 1 - i])
         tab_a = [const.tile([P, 8, P], F32, name="tab_a%d" % kind) for kind in range(2)]
         tab_b = [const.tile([P, 8, 2, 64], F32, name="tab_b%d" % kind) for kind in range(2)]
         rope_q = rope[:].rearrange("p t (j q) -> p t j q", q=4)
-        for kind in range(2):
-            for s, b0, b1 in ((0, 0, 6), (1, 6, 8)):
-                m = 2 * s + kind
-                nb = b1 - b0
-                nc.gpsimd.tensor_tensor(
-                    out=tab_a[kind][:, b0:b1, :].rearrange("p t (j c) -> p t j c", c=2),
-                    in0=rope_q[:, b0:b1, :, 0:4:3],
-                    in1=gain_p[:, m, :, :].unsqueeze(1).to_broadcast([P, nb, 64, 2]),
-                    op=ALU.mult,
-                )
-                nc.gpsimd.tensor_tensor(
-                    out=tab_b[kind][:, b0:b1, :, :],
-                    in0=rope_q[:, b0:b1, :, 1:3].rearrange("p t j c -> p t c j"),
-                    in1=gain_x[:, m, :, :].unsqueeze(1).to_broadcast([P, nb, 2, 64]),
-                    op=ALU.mult,
-                )
 
-        v_codes = {}
+        def tables(kind):
+            if kind >= 0:
+                for s, b0, b1 in ((0, 0, 6), (1, 6, 8)):
+                    m = 2 * s + kind
+                    nb = b1 - b0
+                    nc.gpsimd.tensor_tensor(
+                        out=tab_a[kind][:, b0:b1, :].rearrange("p t (j c) -> p t j c", c=2),
+                        in0=rope_q[:, b0:b1, :, 0:4:3],
+                        in1=gain_p[:, m, :, :].unsqueeze(1).to_broadcast([P, nb, 64, 2]),
+                        op=ALU.mult,
+                    )
+                    for i in range(2):
+                        nc.gpsimd.tensor_tensor(
+                            out=tab_b[kind][:, b0:b1, i, :],
+                            in0=rope_q[:, b0:b1, :, 1 + i],
+                            in1=gain_p[:, m, :, 1 - i].unsqueeze(1).to_broadcast([P, nb, 64]),
+                            op=ALU.mult,
+                        )
 
-        def v_prep(s, c):
+        vst = {}
+
+        def v_open(s, c):
             vg = grps.tile([P, 4096], BF16, name="vg", tag="grp8", align_bytes=64)
-            vg_v = vg[:].bitcast(F32).rearrange("p (g n u) -> p g n u", g=2, u=2)
-            raw = raw_w[(s, 4 + c)]
-            for j in range(4):
-                pool, tag = [(ps_prep, "prep"), (ps_acc, "acc")][(j // 2) % 2]
-                prep(raw[:, j, :], vg_v[:, :, j * P : (j + 1) * P, :], pool, tag, False)
+            vst[("grp", s, c)] = vg
+
+        def v_tr(s, c, j, wide):
+            if wide:
+                bank = ps_y.tile([P, 512], F32, name="bank_v", tag="y")
+            else:
+                bank = ps_prep.tile([P, 512], F32, name="bank_v", tag="prep")
+            words = raw_w[(s, 4 + c)][:, j, :].bitcast(F32)
+            for gu in range(4):
+                nc.tensor.transpose(bank[:, gu * P : (gu + 1) * P], words[:, gu * P : (gu + 1) * P], ident[:])
+            vst[("bank", s, c, j)] = bank
+
+        def v_exit(s, c, j, on_vector):
+            vg_v = vst[("grp", s, c)][:].bitcast(F32).rearrange("p (g n u) -> p g n u", g=2, u=2)
+            src = vst[("bank", s, c, j)][:].rearrange("p (g u n) -> p g n u", g=2, u=2)
+            dst = vg_v[:, :, j * P : (j + 1) * P, :]
+            if on_vector:
+                nc.vector.tensor_copy(out=dst, in_=src)
+            else:
+                nc.scalar.copy(out=dst, in_=src)
+
+        def v_quant(s, c):
             vc = const.tile([P, 1024], U32, name="vc%d%d" % (s, c), align_bytes=64)
             vs = const.tile([P, 1024], U8, name="vs%d%d" % (s, c), align_bytes=64)
-            quant(vc, vs, vg, 0, 1024, 0)
-            v_codes[(s, c)] = (vc, vs)
+            quant(vc, vs, vst[("grp", s, c)], 0, 1024, 0)
+            vst[("codes", s, c)] = (vc, vs)
+            nt = (6, 2)[s]
+            vst[("out", s, c)] = outs.tile([P, 4, nt, P], F32, name="ov%d" % s)
 
-        def v_mult(s, c):
-            vc, vs = v_codes[(s, c)]
-            b0, nt = ((0, 6), (6, 2))[s]
-            ov = outs.tile([P, 4, nt, P], F32, name="ov%d" % s)
-            for t in range(nt):
+        def v_mult(s, c, t, wide):
+            vc, vs = vst[("codes", s, c)]
+            if wide:
                 acc = ps_y.tile([P, 512], F32, name="vacc", tag="y")
-                for g in range(2):
-                    xo = x_word(b0 + t, g)
-                    nc.tensor.matmul_mx(
-                        out=acc[:],
-                        lhsT=x_codes[:, xo : xo + P].bitcast(FP8X4),
-                        lhsT_scale=x_scale[:, xo : xo + P],
-                        rhs=vc[:, g * 512 : (g + 1) * 512].bitcast(FP8X4),
-                        rhs_scale=vs[:, g * 512 : (g + 1) * 512],
-                        start=(g == 0),
-                        stop=(g == 1),
-                    )
-                nc.vector.tensor_tensor(
-                    out=ov[:, :, t, :],
-                    in0=acc[:].rearrange("p (h f) -> p h f", h=4),
-                    in1=vbias[:, s, c * 512 : (c + 1) * 512].rearrange("p (h f) -> p h f", h=4),
-                    op=ALU.add,
+            else:
+                acc = ps_acc.tile([P, 512], F32, name="vacc", tag="acc")
+            for g in range(2):
+                xo = x_word((0, 6)[s] + t, g)
+                nc.tensor.matmul_mx(
+                    out=acc[:],
+                    lhsT=x_codes[:, xo : xo + P].bitcast(FP8X4),
+                    lhsT_scale=x_scale[:, xo : xo + P],
+                    rhs=vc[:, g * 512 : (g + 1) * 512].bitcast(FP8X4),
+                    rhs_scale=vs[:, g * 512 : (g + 1) * 512],
+                    start=(g == 0),
+                    stop=(g == 1),
                 )
+            vst[("acc", s, c, t)] = acc
+
+        def v_add(s, c, t):
+            nc.vector.tensor_tensor(
+                out=vst[("out", s, c)][:, :, t, :],
+                in0=vst[("acc", s, c, t)][:].rearrange("p (h f) -> p h f", h=4),
+                in1=vbias[:, s, c * 512 : (c + 1) * 512].rearrange("p (h f) -> p h f", h=4),
+                op=ALU.add,
+            )
+
+        def v_store(s, c):
             lo, hi = ((256, 1024), (0, 256))[s]
+            nt = (6, 2)[s]
             nc.sync.dma_start(
                 out=out_2[0, 4 * c : 4 * c + 4, lo:hi, :].rearrange("h (p t) f -> p h (t f)", t=nt),
-                in_=ov[:].rearrange("p h t f -> p h (t f)"),
+                in_=vst[("out", s, c)][:].rearrange("p h t f -> p h (t f)"),
             )
 
         st = {}
 
-        def qk_prep(h):
-            grp = grps.tile([P, 2048], BF16, name="grp", tag="grp4", align_bytes=64)
-            grp_v = grp[:].bitcast(F32).rearrange("p (s g n u) -> p s g n u", s=2, g=2, u=2)
-            banks = []
-            for s in range(2):
-                bank = ps_prep.tile([P, 512], F32, name="bank_qk", tag="prep")
-                words = raw_w[(s, h // 4)][:, h % 4, :].bitcast(F32)
-                for gu in range(4):
-                    nc.tensor.transpose(bank[:, gu * P : (gu + 1) * P], words[:, gu * P : (gu + 1) * P], ident[:])
-                banks.append(bank)
-            st[("prep", h)] = (grp, grp_v, banks)
+        def qk_tr(h, s):
+            if s == 0:
+                st[("grp", h)] = grps.tile([P, 2048], BF16, name="grp", tag="grp4", align_bytes=64, bufs=3)
+            bank = ps_prep.tile([P, 512], F32, name="bank_qk", tag="prep")
+            words = raw_w[(s, h // 4)][:, h % 4, :].bitcast(F32)
+            for gu in range(4):
+                nc.tensor.transpose(bank[:, gu * P : (gu + 1) * P], words[:, gu * P : (gu + 1) * P], ident[:])
+            st[("bank", h, s)] = bank
 
-        def qk_exit(h):
-            grp, grp_v, banks = st[("prep", h)]
-            for s in range(2):
-                src = banks[s][:].rearrange("p (g u n) -> p g n u", g=2, u=2)
-                if s == 1 and h % V_EXIT_EVERY == 0:
-                    nc.vector.tensor_copy(out=grp_v[:, s, :, :, :], in_=src)
-                else:
-                    nc.scalar.copy(out=grp_v[:, s, :, :, :], in_=src)
+        def qk_exit(h, s, on_vector):
+            grp_v = st[("grp", h)][:].bitcast(F32).rearrange("p (s g n u) -> p s g n u", s=2, g=2, u=2)
+            src = st[("bank", h, s)][:].rearrange("p (g u n) -> p g n u", g=2, u=2)
+            if on_vector:
+                nc.vector.tensor_copy(out=grp_v[:, s, :, :, :], in_=src)
+            else:
+                nc.scalar.copy(out=grp_v[:, s, :, :, :], in_=src)
 
         def qk_quant(h):
-            grp, grp_v, banks = st[("prep", h)]
             wc = cods.tile([P, 512], U32, name="wc", align_bytes=64)
             ws = cods.tile([P, 512], U8, name="ws", align_bytes=64)
-            quant(wc, ws, grp, 0, 512, 0)
+            quant(wc, ws, st[("grp", h)], 0, 512, 0)
             st[("codes", h)] = (wc, ws)
 
-        def qk_mult(h):
+        PARTS = (((0, 512, 0, 0),), ((0, 256, 0, 1024), (256, 256, 1, 1536)))
+
+        def qk_mult(h, bank):
             wc, ws = st[("codes", h)]
-            accs = [ps_acc.tile([P, 512], F32, name="acc", tag="acc") for b in range(2)]
-            for bank, c0, n, s, xw in ((0, 0, 512, 0, 0), (1, 0, 256, 0, 1024), (1, 256, 256, 1, 1536)):
+            acc = ps_acc.tile([P, 512], F32, name="acc", tag="acc")
+            for c0, n, s, xw in PARTS[bank]:
                 for g in range(2):
                     wo = (2 * s + g) * P
                     xo = xw + g * n
                     nc.tensor.matmul_mx(
-                        out=accs[bank][:, c0 : c0 + n],
+                        out=acc[:, c0 : c0 + n],
                         lhsT=wc[:, wo : wo + P].bitcast(FP8X4),
                         lhsT_scale=ws[:, wo : wo + P],
                         rhs=x_codes[:, xo : xo + n].bitcast(FP8X4),
@@ -275,70 +299,86 @@ def tile_fluxjointattention_pa_kernel(
                         start=(g == 0),
                         stop=(g == 1),
                     )
-            st[("acc", h)] = accs
+            st[("acc", h, bank)] = acc
 
-        def qk_bias(h):
-            accs = st[("acc", h)]
-            yts = [work.tile([P, 512], F32, name="yt") for b in range(2)]
-            for bank, c0, n, s in ((0, 0, 512, 0), (1, 0, 256, 0), (1, 256, 256, 1)):
+        def qk_bias(h, bank):
+            acc = st[("acc", h, bank)]
+            yt = work.tile([P, 512], F32, name="yt")
+            for c0, n, s, xw in PARTS[bank]:
                 nc.scalar.activation(
-                    out=yts[bank][:, c0 : c0 + n],
-                    in_=accs[bank][:, c0 : c0 + n],
+                    out=yt[:, c0 : c0 + n],
+                    in_=acc[:, c0 : c0 + n],
                     func=ACT.Identity,
                     bias=bias_t[:, 16 * s + h : 16 * s + h + 1],
                     scale=1.0,
                 )
-            st[("yt", h)] = yts
+            st[("yt", h, bank)] = yt
 
-        def qk_back(h):
-            yts = st[("yt", h)]
-            ys = []
-            for bank in range(2):
-                y = ps_y.tile([P, 512], F32, name="y", tag="y")
-                for b in range(4):
-                    nc.tensor.transpose(y[:, b * P : (b + 1) * P], yts[bank][:, b * P : (b + 1) * P], ident[:])
-                ys.append(y)
-            st[("y", h)] = ys
+        def qk_back(h, bank):
+            yt = st[("yt", h, bank)]
+            y = ps_y.tile([P, 512], F32, name="y", tag="y")
+            for b in range(4):
+                nc.tensor.transpose(y[:, b * P : (b + 1) * P], yt[:, b * P : (b + 1) * P], ident[:])
+            st[("y", h, bank)] = y
 
-        junk = const.tile([P, P], F32, name="junk")
+        junk = const.tile([P, 8, P], BF16, name="junk")
 
-        def qk_tail(h):
-            ys = st[("y", h)]
-            kind = h // 8
-            o = outs.tile([P, 8, P], F32, name="o", bufs=3)
-            for bank in range(2):
-                y = ys[bank]
-                ss = work.tile([P, 4], F32, name="ss")
-                sd = work.tile([P, 4], F32, name="sd")
-                rs = work.tile([P, 4], F32, name="rs")
-                for b in range(4):
-                    nc.scalar.activation(
-                        out=junk[:], in_=y[:, b * P : (b + 1) * P], func=ACT.Square, accum_out=ss[:, b : b + 1]
-                    )
-                nc.scalar.activation(out=sd[:], in_=ss[:], func=ACT.Sqrt, bias=eps_t[:], scale=1.0 / P)
-                nc.vector.reciprocal(out=rs[:], in_=sd[:])
-                m1 = work.tile([P, 4, P], F32, name="m1")
-                m2 = work.tile([P, 4, 2, 64], F32, name="m2")
-                for b in range(4):
-                    blk = 4 * bank + b
-                    yb = y[:, b * P : (b + 1) * P]
-                    nc.vector.scalar_tensor_tensor(
-                        out=m1[:, b, :], in0=yb, scalar=rs[:, b : b + 1], in1=tab_a[kind][:, blk, :],
-                        op0=ALU.mult, op1=ALU.mult,
-                    )
-                    yp = yb.rearrange("p (j c) -> p j c", c=2)
-                    for i in range(2):
-                        nc.vector.scalar_tensor_tensor(
-                            out=m2[:, b, i, :], in0=yp[:, :, 1 - i], scalar=rs[:, b : b + 1],
-                            in1=tab_b[kind][:, blk, i, :], op0=ALU.mult, op1=ALU.mult,
-                        )
-                nc.gpsimd.tensor_tensor(
-                    out=o[:, 4 * bank : 4 * bank + 4, :].rearrange("p b (j c) -> p b j c", c=2),
-                    in0=m1[:].rearrange("p b (j c) -> p b j c", c=2),
-                    in1=m2[:].rearrange("p b c j -> p b j c"),
-                    op=ALU.add,
+        def qk_square(h, bank):
+            if bank == 0:
+                st[("ss", h)] = work.tile([P, 8], F32, name="ss")
+            y = st[("y", h, bank)]
+            for b in range(4):
+                blk = 4 * bank + b
+                nc.scalar.activation(
+                    out=junk[:, blk, :], in_=y[:, b * P : (b + 1) * P], func=ACT.Square,
+                    accum_out=st[("ss", h)][:, blk : blk + 1],
                 )
-            dst = qk_out[kind]
+
+        def qk_sqrt(h):
+            sd = work.tile([P, 8], F32, name="sd")
+            nc.scalar.activation(out=sd[:], in_=st[("ss", h)][:], func=ACT.Sqrt, bias=eps_t[:], scale=1.0 / P)
+            st[("sd", h)] = sd
+
+        def qk_recip(h):
+            rs = work.tile([P, 8], F32, name="rs")
+            nc.vector.reciprocal(out=rs[:], in_=st[("sd", h)][:])
+            st[("rs", h)] = rs
+
+        def qk_rope(h, bank):
+            y = st[("y", h, bank)]
+            rs = st[("rs", h)]
+            kind = h // 8
+            m1 = work.tile([P, 4, P], F32, name="m1")
+            m2 = work.tile([P, 4, 2, 64], F32, name="m2")
+            for b in range(4):
+                blk = 4 * bank + b
+                yb = y[:, b * P : (b + 1) * P]
+                nc.vector.scalar_tensor_tensor(
+                    out=m1[:, b, :], in0=yb, scalar=rs[:, blk : blk + 1], in1=tab_a[kind][:, blk, :],
+                    op0=ALU.mult, op1=ALU.mult,
+                )
+                yp = yb.rearrange("p (j c) -> p j c", c=2)
+                for i in range(2):
+                    nc.vector.scalar_tensor_tensor(
+                        out=m2[:, b, i, :], in0=yp[:, :, 1 - i], scalar=rs[:, blk : blk + 1],
+                        in1=tab_b[kind][:, blk, i, :], op0=ALU.mult, op1=ALU.mult,
+                    )
+            st[("m", h, bank)] = (m1, m2)
+
+        def qk_add(h, bank):
+            if bank == 0:
+                st[("o", h)] = outs.tile([P, 8, P], F32, name="o", bufs=3)
+            m1, m2 = st[("m", h, bank)]
+            nc.gpsimd.tensor_tensor(
+                out=st[("o", h)][:, 4 * bank : 4 * bank + 4, :].rearrange("p b (j c) -> p b j c", c=2),
+                in0=m1[:].rearrange("p b (j c) -> p b j c", c=2),
+                in1=m2[:].rearrange("p b c j -> p b j c"),
+                op=ALU.add,
+            )
+
+        def qk_store(h):
+            dst = qk_out[h // 8]
+            o = st[("o", h)]
             nc.sync.dma_start(
                 out=dst[0, h % 8, 256:1024, :].rearrange("(p t) f -> p (t f)", t=6),
                 in_=o[:, 0:6, :].rearrange("p t f -> p (t f)"),
@@ -348,37 +388,119 @@ def tile_fluxjointattention_pa_kernel(
                 in_=o[:, 6:8, :].rearrange("p t f -> p (t f)"),
             )
 
-        v_prep(0, 0)
-        load_w(0, 2)
-        v_prep(0, 1)
-        load_w(1, 2)
-        v_mult(0, 0)
-        for h in range(2):
-            qk_prep(h)
-            qk_exit(h)
-            qk_quant(h)
-        v_mult(0, 1)
+        load_x(0)
+        load_x(1)
+        load_v(0, 0, 0, 2)
+        load_v(0, 0, 2, 4)
+        load_x(2)
+        load_x(3)
+        load_v(0, 1, 0, 2)
+        load_v(0, 1, 2, 4)
+        for j in range(2):
+            for s in range(2):
+                load_w(s, 0, j, j + 1)
+        for s in range(2):
+            load_w(s, 0, 2, 4)
+        tables(0)
+
+        def v_back(s, c, t0, t1):
+            for t in range(t0, t1):
+                v_mult(s, c, t, False)
+                v_add(s, c, t)
+
+        def front(h, on_vector):
+            for s in range(2):
+                qk_tr(h, s)
+            qk_exit(h, 0, False)
+            qk_exit(h, 1, on_vector)
+
+        for blk in range(4):
+            x_tr(blk)
+            x_exit(blk, False)
+        x_quant(0)
+        v_open(0, 0)
+        for j in range(4):
+            v_tr(0, 0, j, True)
+            v_exit(0, 0, j, False)
+        for blk in range(4, 8):
+            x_tr(blk)
+            x_exit(blk, False)
+        v_quant(0, 0)
+        x_quant(1)
+        x_quant(2)
+        for s in range(2):
+            load_w(s, 1, 0, 4)
+        v_open(0, 1)
+        for half in range(2):
+            v_back(0, 0, 2 * half, 2 * half + 2)
+            for j in range(2 * half, 2 * half + 2):
+                v_tr(0, 1, j, True)
+                v_exit(0, 1, j, False)
+        load_v(1, 0, 0, 4)
+        v_back(0, 0, 4, 6)
+        v_store(0, 0)
+        front(0, False)
+        front(1, False)
+        qk_quant(0)
+        v_quant(0, 1)
+        load_v(1, 1, 0, 4)
+        bias_columns()
+        tables(1)
         for h in range(NQK + 1):
             if h >= 1:
-                qk_back(h - 1)
-            if h + 2 < NQK:
-                qk_prep(h + 2)
+                qk_back(h - 1, 0)
+                qk_back(h - 1, 1)
             if h < NQK:
-                qk_mult(h)
+                qk_mult(h, 0)
+            if h + 2 < NQK:
+                qk_tr(h + 2, 0)
+                qk_tr(h + 2, 1)
+            elif h < NQK:
+                if h == NQK - 2:
+                    v_open(1, 0)
+                for j in range(2):
+                    v_tr(1, 0, 2 * (h + 2 - NQK) + j, False)
+            if h < NQK:
+                qk_mult(h, 1)
             if h >= 1:
-                qk_tail(h - 1)
+                qk_square(h - 1, 0)
+                qk_square(h - 1, 1)
             if h < NQK:
-                qk_bias(h)
+                qk_bias(h, 0)
+            if h >= 1:
+                qk_sqrt(h - 1)
+            if h < NQK:
+                qk_bias(h, 1)
             if h + 2 < NQK:
-                qk_exit(h + 2)
-                qk_quant(h + 2)
-            if h == 1:
-                load_w(0, 3)
-                load_w(1, 3)
-            if h == 5:
-                load_w(1, 4)
-                load_w(1, 5)
-        v_prep(1, 0)
-        v_prep(1, 1)
-        v_mult(1, 0)
-        v_mult(1, 1)
+                qk_exit(h + 2, 0, False)
+                qk_exit(h + 2, 1, h in V_EXITS)
+            elif h < NQK:
+                for j in range(2):
+                    v_exit(1, 0, 2 * (h + 2 - NQK) + j, False)
+            else:
+                v_open(1, 1)
+                for j in range(4):
+                    v_tr(1, 1, j, False)
+                    v_exit(1, 1, j, False)
+            if h >= 1:
+                qk_recip(h - 1)
+            if h + 1 < NQK:
+                qk_quant(h + 1)
+            elif h == NQK:
+                v_quant(1, 0)
+            if h < FILL:
+                v_back(0, 1, (6 // FILL) * h, (6 // FILL) * (h + 1))
+            if h == FILL - 1:
+                v_store(0, 1)
+            if h >= 1:
+                for bank in range(2):
+                    qk_rope(h - 1, bank)
+                    qk_add(h - 1, bank)
+                qk_store(h - 1)
+            if h in (1, 5):
+                for s in range(2):
+                    load_w(s, (h + 7) // 4, 0, 4)
+        v_quant(1, 1)
+        for c in range(2):
+            v_back(1, c, 0, 2)
+            v_store(1, c)

@@ -18,8 +18,11 @@ K = 1024
 NQK = 16
 EPS = 1e-6
 PIN = True
-V_EXITS = (0, 2, 4, 6, 8, 10, 12)
+V_EXITS = (2, 4, 6, 8, 10, 12)
 FILL = 2
+WARM = 6
+KEEP = 2
+PRE = 2
 
 
 def x_word(blk, g):
@@ -53,7 +56,7 @@ def tile_fluxjointattention_pa_kernel(
             ctx.enter_context(tc.manual_schedule())
         const = ctx.enter_context(tc.tile_pool(name="const", bufs=1))
         raws = ctx.enter_context(tc.tile_pool(name="raws", bufs=4))
-        grps = ctx.enter_context(tc.tile_pool(name="grps", bufs=2))
+        grps = ctx.enter_context(tc.tile_pool(name="grps", bufs=3))
         cods = ctx.enter_context(tc.tile_pool(name="cods", bufs=4))
         work = ctx.enter_context(tc.tile_pool(name="work", bufs=4))
         outs = ctx.enter_context(tc.tile_pool(name="outs", bufs=2))
@@ -96,6 +99,17 @@ def tile_fluxjointattention_pa_kernel(
             )
         nc.gpsimd.dma_start(out=vbias[:, 1, :], in_=biases[1][2048:3072].partition_broadcast(P))
 
+        zero_b = const.tile([P, 512], BF16, name="zero_b", align_bytes=64)
+        nc.vector.memset(zero_b[:], 0.0)
+        zero_w = const.tile([P, P], U32, name="zero_w", align_bytes=64)
+        one_s = const.tile([P, P], U8, name="one_s", align_bytes=64)
+        nc.vector.quantize_mx(out=zero_w[:].bitcast(FP8X4), scales=one_s[:], in_=zero_b[:])
+        idle_ps = ps_acc.tile([P, 512], F32, name="idle_ps", tag="acc")
+
+        def idle_passes(n):
+            for i in range(n):
+                nc.tensor.matmul(out=idle_ps[:], lhsT=zero_b[:, 0:P], rhs=zero_b[:], start=True, stop=True)
+
         raw_w = {}
 
         def load_w(s, chunk, j0, j1):
@@ -130,7 +144,7 @@ def tile_fluxjointattention_pa_kernel(
             nc.sync.dma_start(out=raw_x[pair // 2][:, 2 * (pair % 2) : 2 * (pair % 2) + 2, :], in_=src)
 
         def x_tr(blk):
-            pool, tag = ((ps_prep, "prep"), (ps_acc, "acc"), (ps_y, "y"), (ps_y, "y"))[blk // 2]
+            pool, tag = ((ps_prep, "prep"), (ps_y, "y"), (ps_y, "y"), (ps_prep, "prep"))[blk // 2]
             bank = pool.tile([P, 512], F32, name="bank_x", tag=tag)
             words = raw_x[blk // 4][:, blk % 4, :].bitcast(F32)
             for gu in range(4):
@@ -287,6 +301,15 @@ def tile_fluxjointattention_pa_kernel(
             wc, ws = st[("codes", h)]
             acc = ps_acc.tile([P, 512], F32, name="acc", tag="acc")
             for c0, n, s, xw in PARTS[bank]:
+                nc.tensor.matmul_mx(
+                    out=acc[:, c0 : c0 + n],
+                    lhsT=zero_w[:].bitcast(FP8X4),
+                    lhsT_scale=one_s[:],
+                    rhs=x_codes[:, xw : xw + n].bitcast(FP8X4),
+                    rhs_scale=x_scale[:, xw : xw + n],
+                    start=True,
+                    stop=False,
+                )
                 for g in range(2):
                     wo = (2 * s + g) * P
                     xo = xw + g * n
@@ -296,7 +319,7 @@ def tile_fluxjointattention_pa_kernel(
                         lhsT_scale=ws[:, wo : wo + P],
                         rhs=x_codes[:, xo : xo + n].bitcast(FP8X4),
                         rhs_scale=x_scale[:, xo : xo + n],
-                        start=(g == 0),
+                        start=False,
                         stop=(g == 1),
                     )
             st[("acc", h, bank)] = acc
@@ -414,42 +437,55 @@ def tile_fluxjointattention_pa_kernel(
             qk_exit(h, 0, False)
             qk_exit(h, 1, on_vector)
 
+        idle_passes(WARM)
         for blk in range(4):
             x_tr(blk)
             x_exit(blk, False)
+            if blk % 2 == 1:
+                idle_passes(KEEP)
         x_quant(0)
         v_open(0, 0)
         for j in range(4):
-            v_tr(0, 0, j, True)
+            v_tr(0, 0, j, j < 2)
             v_exit(0, 0, j, False)
+            if j % 2 == 1:
+                idle_passes(KEEP)
         for blk in range(4, 8):
             x_tr(blk)
             x_exit(blk, False)
+            if blk % 2 == 1:
+                idle_passes(KEEP)
         v_quant(0, 0)
         x_quant(1)
         x_quant(2)
         for s in range(2):
             load_w(s, 1, 0, 4)
+        v_back(0, 0, 0, 2)
         v_open(0, 1)
-        for half in range(2):
-            v_back(0, 0, 2 * half, 2 * half + 2)
-            for j in range(2 * half, 2 * half + 2):
-                v_tr(0, 1, j, True)
-                v_exit(0, 1, j, False)
+        for j in range(4):
+            v_tr(0, 1, j, True)
+            v_exit(0, 1, j, False)
         load_v(1, 0, 0, 4)
-        v_back(0, 0, 4, 6)
-        v_store(0, 0)
-        front(0, False)
-        front(1, False)
+        bias_columns()
+        v_back(0, 0, 2, 4)
+        front(0, True)
         qk_quant(0)
         v_quant(0, 1)
         load_v(1, 1, 0, 4)
-        bias_columns()
+        v_back(0, 0, 4, 6)
+        v_store(0, 0)
+        front(1, True)
+        qk_mult(0, 0)
+        qk_mult(0, 1)
+        qk_bias(0, 0)
+        qk_bias(0, 1)
+        qk_quant(1)
+        v_back(0, 1, 0, PRE)
+        front(2, False)
         tables(1)
-        for h in range(NQK + 1):
-            if h >= 1:
-                qk_back(h - 1, 0)
-                qk_back(h - 1, 1)
+        for h in range(1, NQK + 1):
+            qk_back(h - 1, 0)
+            qk_back(h - 1, 1)
             if h < NQK:
                 qk_mult(h, 0)
             if h + 2 < NQK:
@@ -462,13 +498,11 @@ def tile_fluxjointattention_pa_kernel(
                     v_tr(1, 0, 2 * (h + 2 - NQK) + j, False)
             if h < NQK:
                 qk_mult(h, 1)
-            if h >= 1:
-                qk_square(h - 1, 0)
-                qk_square(h - 1, 1)
+            qk_square(h - 1, 0)
+            qk_square(h - 1, 1)
             if h < NQK:
                 qk_bias(h, 0)
-            if h >= 1:
-                qk_sqrt(h - 1)
+            qk_sqrt(h - 1)
             if h < NQK:
                 qk_bias(h, 1)
             if h + 2 < NQK:
@@ -482,21 +516,19 @@ def tile_fluxjointattention_pa_kernel(
                 for j in range(4):
                     v_tr(1, 1, j, False)
                     v_exit(1, 1, j, False)
-            if h >= 1:
-                qk_recip(h - 1)
+            qk_recip(h - 1)
             if h + 1 < NQK:
                 qk_quant(h + 1)
             elif h == NQK:
                 v_quant(1, 0)
-            if h < FILL:
-                v_back(0, 1, (6 // FILL) * h, (6 // FILL) * (h + 1))
-            if h == FILL - 1:
+            if h <= FILL:
+                v_back(0, 1, PRE + ((6 - PRE) // FILL) * (h - 1), PRE + ((6 - PRE) // FILL) * h)
+            if h == FILL:
                 v_store(0, 1)
-            if h >= 1:
-                for bank in range(2):
-                    qk_rope(h - 1, bank)
-                    qk_add(h - 1, bank)
-                qk_store(h - 1)
+            for bank in range(2):
+                qk_rope(h - 1, bank)
+                qk_add(h - 1, bank)
+            qk_store(h - 1)
             if h in (1, 5):
                 for s in range(2):
                     load_w(s, (h + 7) // 4, 0, 4)

@@ -18,7 +18,7 @@ K = 1024
 NQK = 16
 EPS = 1e-6
 PIN = True
-V_EXITS = (2, 4, 6, 8, 10, 12)
+V_EXITS = (1, 2, 3, 4, 5, 6, 7, 8, 9, 10, 11, 12, 13)
 FILL = 2
 WARM = 6
 KEEP = 2
@@ -101,9 +101,6 @@ def tile_fluxjointattention_pa_kernel(
 
         zero_b = const.tile([P, 512], BF16, name="zero_b", align_bytes=64)
         nc.vector.memset(zero_b[:], 0.0)
-        zero_w = const.tile([P, P], U32, name="zero_w", align_bytes=64)
-        one_s = const.tile([P, P], U8, name="one_s", align_bytes=64)
-        nc.vector.quantize_mx(out=zero_w[:].bitcast(FP8X4), scales=one_s[:], in_=zero_b[:])
         idle_ps = ps_acc.tile([P, 512], F32, name="idle_ps", tag="acc")
 
         def idle_passes(n):
@@ -179,8 +176,7 @@ def tile_fluxjointattention_pa_kernel(
             nc.vector.tensor_copy(out=bias_t[:], in_=bias_ps[:, 0:32])
 
         gain_p = gain[:].rearrange("p m (j c) -> p m j c", c=2)
-        tab_a = [const.tile([P, 8, P], F32, name="tab_a%d" % kind) for kind in range(2)]
-        tab_b = [const.tile([P, 8, 2, 64], F32, name="tab_b%d" % kind) for kind in range(2)]
+        tab = [const.tile([P, 8, 2, P], F32, name="tab%d" % kind) for kind in range(2)]
         rope_q = rope[:].rearrange("p t (j q) -> p t j q", q=4)
 
         def tables(kind):
@@ -189,18 +185,17 @@ def tile_fluxjointattention_pa_kernel(
                     m = 2 * s + kind
                     nb = b1 - b0
                     nc.gpsimd.tensor_tensor(
-                        out=tab_a[kind][:, b0:b1, :].rearrange("p t (j c) -> p t j c", c=2),
+                        out=tab[kind][:, b0:b1, 0, :].rearrange("p t (j c) -> p t j c", c=2),
                         in0=rope_q[:, b0:b1, :, 0:4:3],
                         in1=gain_p[:, m, :, :].unsqueeze(1).to_broadcast([P, nb, 64, 2]),
                         op=ALU.mult,
                     )
-                    for i in range(2):
-                        nc.gpsimd.tensor_tensor(
-                            out=tab_b[kind][:, b0:b1, i, :],
-                            in0=rope_q[:, b0:b1, :, 1 + i],
-                            in1=gain_p[:, m, :, 1 - i].unsqueeze(1).to_broadcast([P, nb, 64]),
-                            op=ALU.mult,
-                        )
+                    nc.gpsimd.tensor_tensor(
+                        out=tab[kind][:, b0:b1, 1, :].rearrange("p t (j c) -> p t j c", c=2),
+                        in0=rope_q[:, b0:b1, :, 2:0:-1],
+                        in1=gain_p[:, m, :, :].unsqueeze(1).to_broadcast([P, nb, 64, 2]),
+                        op=ALU.mult,
+                    )
 
         vst = {}
 
@@ -301,15 +296,6 @@ def tile_fluxjointattention_pa_kernel(
             wc, ws = st[("codes", h)]
             acc = ps_acc.tile([P, 512], F32, name="acc", tag="acc")
             for c0, n, s, xw in PARTS[bank]:
-                nc.tensor.matmul_mx(
-                    out=acc[:, c0 : c0 + n],
-                    lhsT=zero_w[:].bitcast(FP8X4),
-                    lhsT_scale=one_s[:],
-                    rhs=x_codes[:, xw : xw + n].bitcast(FP8X4),
-                    rhs_scale=x_scale[:, xw : xw + n],
-                    start=True,
-                    stop=False,
-                )
                 for g in range(2):
                     wo = (2 * s + g) * P
                     xo = xw + g * n
@@ -319,7 +305,7 @@ def tile_fluxjointattention_pa_kernel(
                         lhsT_scale=ws[:, wo : wo + P],
                         rhs=x_codes[:, xo : xo + n].bitcast(FP8X4),
                         rhs_scale=x_scale[:, xo : xo + n],
-                        start=False,
+                        start=(g == 0),
                         stop=(g == 1),
                     )
             st[("acc", h, bank)] = acc
@@ -371,31 +357,27 @@ def tile_fluxjointattention_pa_kernel(
             y = st[("y", h, bank)]
             rs = st[("rs", h)]
             kind = h // 8
-            m1 = work.tile([P, 4, P], F32, name="m1")
-            m2 = work.tile([P, 4, 2, 64], F32, name="m2")
+            mw = work.tile([P, 4, 2, P], F32, name="mw")
             for b in range(4):
                 blk = 4 * bank + b
-                yb = y[:, b * P : (b + 1) * P]
                 nc.vector.scalar_tensor_tensor(
-                    out=m1[:, b, :], in0=yb, scalar=rs[:, blk : blk + 1], in1=tab_a[kind][:, blk, :],
-                    op0=ALU.mult, op1=ALU.mult,
+                    out=mw[:, b, :, :],
+                    in0=y[:, b * P : (b + 1) * P].unsqueeze(1).to_broadcast([P, 2, P]),
+                    scalar=rs[:, blk : blk + 1],
+                    in1=tab[kind][:, blk, :, :],
+                    op0=ALU.mult,
+                    op1=ALU.mult,
                 )
-                yp = yb.rearrange("p (j c) -> p j c", c=2)
-                for i in range(2):
-                    nc.vector.scalar_tensor_tensor(
-                        out=m2[:, b, i, :], in0=yp[:, :, 1 - i], scalar=rs[:, blk : blk + 1],
-                        in1=tab_b[kind][:, blk, i, :], op0=ALU.mult, op1=ALU.mult,
-                    )
-            st[("m", h, bank)] = (m1, m2)
+            st[("m", h, bank)] = mw
 
         def qk_add(h, bank):
             if bank == 0:
                 st[("o", h)] = outs.tile([P, 8, P], F32, name="o", bufs=3)
-            m1, m2 = st[("m", h, bank)]
+            mw = st[("m", h, bank)]
             nc.gpsimd.tensor_tensor(
                 out=st[("o", h)][:, 4 * bank : 4 * bank + 4, :].rearrange("p b (j c) -> p b j c", c=2),
-                in0=m1[:].rearrange("p b (j c) -> p b j c", c=2),
-                in1=m2[:].rearrange("p b c j -> p b j c"),
+                in0=mw[:, :, 0, :].rearrange("p b (j c) -> p b j c", c=2),
+                in1=mw[:, :, 1, :].rearrange("p b (j c) -> p b j c", c=2)[:, :, :, ::-1],
                 op=ALU.add,
             )
 

@@ -18,7 +18,7 @@ K = 1024
 NQK = 16
 EPS = 1e-6
 PIN = True
-V_EXITS = (1, 2, 3, 4, 5, 6, 7, 8, 9, 10, 11, 12, 13)
+V_EXITS = (99,)
 FILL = 2
 WARM = 6
 KEEP = 2
@@ -374,7 +374,7 @@ def tile_fluxjointattention_pa_kernel(
             if bank == 0:
                 st[("o", h)] = outs.tile([P, 8, P], F32, name="o", bufs=3)
             mw = st[("m", h, bank)]
-            nc.gpsimd.tensor_tensor(
+            nc.vector.tensor_tensor(
                 out=st[("o", h)][:, 4 * bank : 4 * bank + 4, :].rearrange("p b (j c) -> p b j c", c=2),
                 in0=mw[:, :, 0, :].rearrange("p b (j c) -> p b j c", c=2),
                 in1=mw[:, :, 1, :].rearrange("p b (j c) -> p b j c", c=2)[:, :, :, ::-1],
@@ -509,6 +509,7 @@ def tile_fluxjointattention_pa_kernel(
                 v_store(0, 1)
             for bank in range(2):
                 qk_rope(h - 1, bank)
+            for bank in range(2):
                 qk_add(h - 1, bank)
             qk_store(h - 1)
             if h in (1, 5):

@@ -20,9 +20,10 @@ EPS = 1e-6
 PIN = True
 V_EXITS = (99,)
 FILL = 2
-WARM = 6
-KEEP = 2
+WARM = 0
+KEEP = 0
 PRE = 2
+BACK_MM = 2
 
 
 def x_word(blk, g):
@@ -99,14 +100,6 @@ def tile_fluxjointattention_pa_kernel(
             )
         nc.gpsimd.dma_start(out=vbias[:, 1, :], in_=biases[1][2048:3072].partition_broadcast(P))
 
-        zero_b = const.tile([P, 512], BF16, name="zero_b", align_bytes=64)
-        nc.vector.memset(zero_b[:], 0.0)
-        idle_ps = ps_acc.tile([P, 512], F32, name="idle_ps", tag="acc")
-
-        def idle_passes(n):
-            for i in range(n):
-                nc.tensor.matmul(out=idle_ps[:], lhsT=zero_b[:, 0:P], rhs=zero_b[:], start=True, stop=True)
-
         raw_w = {}
 
         def load_w(s, chunk, j0, j1):
@@ -170,10 +163,10 @@ def tile_fluxjointattention_pa_kernel(
 
         def bias_columns():
             brow_f = const.tile([P, P], F32, name="brow_f")
-            nc.vector.tensor_copy(out=brow_f[:], in_=brow[:])
+            nc.scalar.copy(out=brow_f[:], in_=brow[:])
             bias_ps = ps_prep.tile([P, 512], F32, name="bias_ps", tag="prep")
             nc.tensor.transpose(bias_ps[:, 0:P], brow_f[:], ident[:])
-            nc.vector.tensor_copy(out=bias_t[:], in_=bias_ps[:, 0:32])
+            nc.scalar.copy(out=bias_t[:], in_=bias_ps[:, 0:32])
 
         gain_p = gain[:].rearrange("p m (j c) -> p m j c", c=2)
         tab = [const.tile([P, 8, 2, P], F32, name="tab%d" % kind) for kind in range(2)]
@@ -327,7 +320,12 @@ def tile_fluxjointattention_pa_kernel(
             yt = st[("yt", h, bank)]
             y = ps_y.tile([P, 512], F32, name="y", tag="y")
             for b in range(4):
-                nc.tensor.transpose(y[:, b * P : (b + 1) * P], yt[:, b * P : (b + 1) * P], ident[:])
+                if b < BACK_MM:
+                    nc.tensor.matmul(
+                        out=y[:, b * P : (b + 1) * P], lhsT=yt[:, b * P : (b + 1) * P], rhs=ident[:], start=True, stop=True
+                    )
+                else:
+                    nc.tensor.transpose(y[:, b * P : (b + 1) * P], yt[:, b * P : (b + 1) * P], ident[:])
             st[("y", h, bank)] = y
 
         junk = const.tile([P, 8, P], BF16, name="junk")
@@ -413,56 +411,62 @@ def tile_fluxjointattention_pa_kernel(
                 v_mult(s, c, t, False)
                 v_add(s, c, t)
 
+        def v_wide(s, c, t0, t1):
+            for t in range(t0, t1):
+                v_mult(s, c, t, True)
+            for t in range(t0, t1):
+                v_add(s, c, t)
+
         def front(h, on_vector):
             for s in range(2):
                 qk_tr(h, s)
             qk_exit(h, 0, False)
             qk_exit(h, 1, on_vector)
 
-        idle_passes(WARM)
         for blk in range(4):
             x_tr(blk)
             x_exit(blk, False)
-            if blk % 2 == 1:
-                idle_passes(KEEP)
         x_quant(0)
         v_open(0, 0)
         for j in range(4):
             v_tr(0, 0, j, j < 2)
             v_exit(0, 0, j, False)
-            if j % 2 == 1:
-                idle_passes(KEEP)
+        v_quant(0, 0)
         for blk in range(4, 8):
             x_tr(blk)
             x_exit(blk, False)
-            if blk % 2 == 1:
-                idle_passes(KEEP)
-        v_quant(0, 0)
         x_quant(1)
         x_quant(2)
         for s in range(2):
             load_w(s, 1, 0, 4)
-        v_back(0, 0, 0, 2)
+        v_wide(0, 0, 0, 2)
         v_open(0, 1)
         for j in range(4):
-            v_tr(0, 1, j, True)
+            v_tr(0, 1, j, False)
             v_exit(0, 1, j, False)
         load_v(1, 0, 0, 4)
-        bias_columns()
-        v_back(0, 0, 2, 4)
-        front(0, True)
-        qk_quant(0)
+        v_wide(0, 0, 2, 6)
+        v_store(0, 0)
         v_quant(0, 1)
         load_v(1, 1, 0, 4)
-        v_back(0, 0, 4, 6)
-        v_store(0, 0)
-        front(1, True)
+        bias_columns()
+        front(0, False)
+        front(1, False)
+        for t in range(3):
+            v_mult(0, 1, t, True)
+        qk_quant(0)
+        for t in range(3):
+            v_add(0, 1, t)
         qk_mult(0, 0)
         qk_mult(0, 1)
         qk_bias(0, 0)
         qk_bias(0, 1)
+        for t in range(3, 6):
+            v_mult(0, 1, t, True)
         qk_quant(1)
-        v_back(0, 1, 0, PRE)
+        for t in range(3, 6):
+            v_add(0, 1, t)
+        v_store(0, 1)
         front(2, False)
         tables(1)
         for h in range(1, NQK + 1):
@@ -503,10 +507,6 @@ def tile_fluxjointattention_pa_kernel(
                 qk_quant(h + 1)
             elif h == NQK:
                 v_quant(1, 0)
-            if h <= FILL:
-                v_back(0, 1, PRE + ((6 - PRE) // FILL) * (h - 1), PRE + ((6 - PRE) // FILL) * h)
-            if h == FILL:
-                v_store(0, 1)
             for bank in range(2):
                 qk_rope(h - 1, bank)
             for bank in range(2):

@@ -15,23 +15,19 @@ ALU = mybir.AluOpType
 
 P = 128
 K = 1024
-NQK = 16
+HEADS = 16
 EPS = 1e-6
-PIN = True
-V_EXITS = (99,)
-FILL = 2
-WARM = 0
-KEEP = 0
-PRE = 2
-BACK_MM = 2
+TOKEN_BLOCKS = (6, 2)
+FIRST_BLOCK = (0, 6)
+BANK_PARTS = (((0, 512, 0, 0),), ((0, 256, 0, 1024), (256, 256, 1, 1536)))
 
 
 def x_word(blk, g):
     if blk < 4:
-        return g * 512 + blk * 128
+        return g * 512 + blk * P
     if blk < 6:
-        return 1024 + g * 256 + (blk - 4) * 128
-    return 1536 + g * 256 + (blk - 6) * 128
+        return 1024 + g * 256 + (blk - 4) * P
+    return 1536 + g * 256 + (blk - 6) * P
 
 
 def tile_fluxjointattention_pa_kernel(
@@ -53,8 +49,7 @@ def tile_fluxjointattention_pa_kernel(
 ):
     nc = tc.nc
     with ExitStack() as ctx:
-        if PIN:
-            ctx.enter_context(tc.manual_schedule())
+        ctx.enter_context(tc.manual_schedule())
         const = ctx.enter_context(tc.tile_pool(name="const", bufs=1))
         raws = ctx.enter_context(tc.tile_pool(name="raws", bufs=4))
         grps = ctx.enter_context(tc.tile_pool(name="grps", bufs=3))
@@ -88,31 +83,27 @@ def tile_fluxjointattention_pa_kernel(
         vbias = const.tile([P, 2, 1024], BF16, name="vbias")
         rope = const.tile([P, 8, 256], BF16, name="rope")
         gain = const.tile([P, 4, P], BF16, name="gain")
-        nc.gpsimd.dma_start(out=vbias[:, 0, :], in_=biases[0][2048:3072].partition_broadcast(P))
-        nc.gpsimd.dma_start(out=rope[:, 0:6, :], in_=rope_v[256:1024, :].rearrange("(p t) e -> p t e", t=6))
-        nc.gpsimd.dma_start(out=rope[:, 6:8, :], in_=rope_v[0:256, :].rearrange("(p t) e -> p t e", t=2))
-        for m in (0, 2, 1, 3):
-            nc.gpsimd.dma_start(out=gain[:, m, :], in_=gains[m].partition_broadcast(P))
         for s in range(2):
             nc.gpsimd.dma_start(
                 out=brow[16 * s : 16 * s + 16, :],
                 in_=biases[s][0:2048].rearrange("(r f) -> r f", f=P),
             )
+        nc.gpsimd.dma_start(out=vbias[:, 0, :], in_=biases[0][2048:3072].partition_broadcast(P))
+        nc.gpsimd.dma_start(out=rope[:, 0:6, :], in_=rope_v[256:1024, :].rearrange("(p t) e -> p t e", t=6))
+        nc.gpsimd.dma_start(out=rope[:, 6:8, :], in_=rope_v[0:256, :].rearrange("(p t) e -> p t e", t=2))
+        for m in (0, 2, 1, 3):
+            nc.gpsimd.dma_start(out=gain[:, m, :], in_=gains[m].partition_broadcast(P))
         nc.gpsimd.dma_start(out=vbias[:, 1, :], in_=biases[1][2048:3072].partition_broadcast(P))
 
-        raw_w = {}
+        def turn(pool, tag, rows):
+            bank = pool.tile([P, 512], F32, name="bank_" + tag, tag=tag)
+            words = rows.bitcast(F32)
+            for gu in range(4):
+                nc.tensor.transpose(bank[:, gu * P : (gu + 1) * P], words[:, gu * P : (gu + 1) * P], ident[:])
+            return bank
 
-        def load_w(s, chunk, j0, j1):
-            if j0 == 0:
-                raw_w[(s, chunk)] = raws.tile([P, 4, K], BF16, name="raw_w%d_%d" % (s, chunk), tag="raw")
-            nc.sync.dma_start(out=raw_w[(s, chunk)][:, j0:j1, :], in_=w_v[s][:, 4 * chunk + j0 : 4 * chunk + j1, :])
-
-        def load_v(s, c, j0, j1):
-            if j0 == 0:
-                raw_w[(s, 4 + c)] = raws.tile([P, 4, K], BF16, name="raw_v%d_%d" % (s, c), tag="rawv", bufs=2)
-            nc.sync.dma_start(
-                out=raw_w[(s, 4 + c)][:, j0:j1, :], in_=w_v[s][:, 16 + 4 * c + j0 : 16 + 4 * c + j1, :]
-            )
+        def leave(bank, dst):
+            nc.scalar.copy(out=dst, in_=bank[:].rearrange("p (g u n) -> p g n u", g=2, u=2))
 
         def quant(codes, scales, grp, w0, w1, g0):
             nc.vector.quantize_mx(
@@ -121,37 +112,35 @@ def tile_fluxjointattention_pa_kernel(
                 in_=grp[:, g0 : g0 + 4 * (w1 - w0)],
             )
 
+        raw_w = {}
+
+        def load_w(s, chunk, j0, j1):
+            if j0 == 0:
+                if chunk < 4:
+                    raw_w[(s, chunk)] = raws.tile([P, 4, K], BF16, name="raw_w%d_%d" % (s, chunk), tag="raw")
+                else:
+                    raw_w[(s, chunk)] = raws.tile([P, 4, K], BF16, name="raw_w%d_%d" % (s, chunk), tag="rawv", bufs=2)
+            nc.sync.dma_start(out=raw_w[(s, chunk)][:, j0:j1, :], in_=w_v[s][:, 4 * chunk + j0 : 4 * chunk + j1, :])
+
         raw_x = [raws.tile([P, 4, K], BF16, name="raw_x%d" % i, tag="raw") for i in range(2)]
         x_codes = const.tile([P, 2048], U32, name="x_codes", align_bytes=64)
         x_scale = const.tile([P, 2048], U8, name="x_scale", align_bytes=64)
         xg = [grps.tile([P, 4096], BF16, name="xg%d" % i, tag="grp8", align_bytes=64) for i in range(2)]
         xg0_v = xg[0][:].bitcast(F32).rearrange("p (g n u) -> p g n u", g=2, u=2)
         xg1_v = xg[1][:].bitcast(F32).rearrange("p (c g n u) -> p c g n u", c=2, g=2, u=2)
-        x_bank = {}
 
         def load_x(pair):
             src = (xa_v[:, 0:2, :], xa_v[:, 2:4, :], xa_v[:, 4:6, :], xb_v)[pair]
             nc.sync.dma_start(out=raw_x[pair // 2][:, 2 * (pair % 2) : 2 * (pair % 2) + 2, :], in_=src)
 
-        def x_tr(blk):
+        def x_prep(blk):
             pool, tag = ((ps_prep, "prep"), (ps_y, "y"), (ps_y, "y"), (ps_prep, "prep"))[blk // 2]
-            bank = pool.tile([P, 512], F32, name="bank_x", tag=tag)
-            words = raw_x[blk // 4][:, blk % 4, :].bitcast(F32)
-            for gu in range(4):
-                nc.tensor.transpose(bank[:, gu * P : (gu + 1) * P], words[:, gu * P : (gu + 1) * P], ident[:])
-            x_bank[blk] = bank
-
-        def x_exit(blk, on_vector):
+            bank = turn(pool, tag, raw_x[blk // 4][:, blk % 4, :])
             if blk < 4:
-                dst = xg0_v[:, :, blk * P : (blk + 1) * P, :]
+                leave(bank, xg0_v[:, :, blk * P : (blk + 1) * P, :])
             else:
                 c, tb = divmod(blk - 4, 2)
-                dst = xg1_v[:, c, :, tb * P : (tb + 1) * P, :]
-            src = x_bank[blk][:].rearrange("p (g u n) -> p g n u", g=2, u=2)
-            if on_vector:
-                nc.vector.tensor_copy(out=dst, in_=src)
-            else:
-                nc.scalar.copy(out=dst, in_=src)
+                leave(bank, xg1_v[:, c, :, tb * P : (tb + 1) * P, :])
 
         def x_quant(c):
             if c == 0:
@@ -173,64 +162,51 @@ def tile_fluxjointattention_pa_kernel(
         rope_q = rope[:].rearrange("p t (j q) -> p t j q", q=4)
 
         def tables(kind):
-            if kind >= 0:
-                for s, b0, b1 in ((0, 0, 6), (1, 6, 8)):
-                    m = 2 * s + kind
-                    nb = b1 - b0
-                    nc.gpsimd.tensor_tensor(
-                        out=tab[kind][:, b0:b1, 0, :].rearrange("p t (j c) -> p t j c", c=2),
-                        in0=rope_q[:, b0:b1, :, 0:4:3],
-                        in1=gain_p[:, m, :, :].unsqueeze(1).to_broadcast([P, nb, 64, 2]),
-                        op=ALU.mult,
-                    )
-                    nc.gpsimd.tensor_tensor(
-                        out=tab[kind][:, b0:b1, 1, :].rearrange("p t (j c) -> p t j c", c=2),
-                        in0=rope_q[:, b0:b1, :, 2:0:-1],
-                        in1=gain_p[:, m, :, :].unsqueeze(1).to_broadcast([P, nb, 64, 2]),
-                        op=ALU.mult,
-                    )
+            for s in range(2):
+                b0 = FIRST_BLOCK[s]
+                b1 = b0 + TOKEN_BLOCKS[s]
+                g_bc = gain_p[:, 2 * s + kind, :, :].unsqueeze(1).to_broadcast([P, b1 - b0, 64, 2])
+                nc.vector.tensor_tensor(
+                    out=tab[kind][:, b0:b1, 0, :].rearrange("p t (j c) -> p t j c", c=2),
+                    in0=rope_q[:, b0:b1, :, 0:4:3],
+                    in1=g_bc,
+                    op=ALU.mult,
+                )
+                nc.vector.tensor_tensor(
+                    out=tab[kind][:, b0:b1, 1, :].rearrange("p t (j c) -> p t j c", c=2),
+                    in0=rope_q[:, b0:b1, :, 2:0:-1],
+                    in1=g_bc,
+                    op=ALU.mult,
+                )
 
         vst = {}
 
         def v_open(s, c):
-            vg = grps.tile([P, 4096], BF16, name="vg", tag="grp8", align_bytes=64)
-            vst[("grp", s, c)] = vg
+            vst[("grp", s, c)] = grps.tile([P, 4096], BF16, name="vg", tag="grp8", align_bytes=64)
 
-        def v_tr(s, c, j, wide):
-            if wide:
-                bank = ps_y.tile([P, 512], F32, name="bank_v", tag="y")
-            else:
-                bank = ps_prep.tile([P, 512], F32, name="bank_v", tag="prep")
-            words = raw_w[(s, 4 + c)][:, j, :].bitcast(F32)
-            for gu in range(4):
-                nc.tensor.transpose(bank[:, gu * P : (gu + 1) * P], words[:, gu * P : (gu + 1) * P], ident[:])
-            vst[("bank", s, c, j)] = bank
+        def v_turn(s, c, j, pool, tag):
+            vst[("bank", s, c, j)] = turn(pool, tag, raw_w[(s, 4 + c)][:, j, :])
 
-        def v_exit(s, c, j, on_vector):
+        def v_leave(s, c, j):
             vg_v = vst[("grp", s, c)][:].bitcast(F32).rearrange("p (g n u) -> p g n u", g=2, u=2)
-            src = vst[("bank", s, c, j)][:].rearrange("p (g u n) -> p g n u", g=2, u=2)
-            dst = vg_v[:, :, j * P : (j + 1) * P, :]
-            if on_vector:
-                nc.vector.tensor_copy(out=dst, in_=src)
-            else:
-                nc.scalar.copy(out=dst, in_=src)
+            leave(vst[("bank", s, c, j)], vg_v[:, :, j * P : (j + 1) * P, :])
+
+        def v_prep(s, c, j, pool, tag):
+            v_turn(s, c, j, pool, tag)
+            v_leave(s, c, j)
 
         def v_quant(s, c):
             vc = const.tile([P, 1024], U32, name="vc%d%d" % (s, c), align_bytes=64)
             vs = const.tile([P, 1024], U8, name="vs%d%d" % (s, c), align_bytes=64)
             quant(vc, vs, vst[("grp", s, c)], 0, 1024, 0)
             vst[("codes", s, c)] = (vc, vs)
-            nt = (6, 2)[s]
-            vst[("out", s, c)] = outs.tile([P, 4, nt, P], F32, name="ov%d" % s)
+            vst[("out", s, c)] = outs.tile([P, 4, TOKEN_BLOCKS[s], P], F32, name="ov%d" % s)
 
-        def v_mult(s, c, t, wide):
+        def v_mult(s, c, t, pool, tag):
             vc, vs = vst[("codes", s, c)]
-            if wide:
-                acc = ps_y.tile([P, 512], F32, name="vacc", tag="y")
-            else:
-                acc = ps_acc.tile([P, 512], F32, name="vacc", tag="acc")
+            acc = pool.tile([P, 512], F32, name="vacc", tag=tag)
             for g in range(2):
-                xo = x_word((0, 6)[s] + t, g)
+                xo = x_word(FIRST_BLOCK[s] + t, g)
                 nc.tensor.matmul_mx(
                     out=acc[:],
                     lhsT=x_codes[:, xo : xo + P].bitcast(FP8X4),
@@ -252,30 +228,33 @@ def tile_fluxjointattention_pa_kernel(
 
         def v_store(s, c):
             lo, hi = ((256, 1024), (0, 256))[s]
-            nt = (6, 2)[s]
             nc.sync.dma_start(
-                out=out_2[0, 4 * c : 4 * c + 4, lo:hi, :].rearrange("h (p t) f -> p h (t f)", t=nt),
+                out=out_2[0, 4 * c : 4 * c + 4, lo:hi, :].rearrange("h (p t) f -> p h (t f)", t=TOKEN_BLOCKS[s]),
                 in_=vst[("out", s, c)][:].rearrange("p h t f -> p h (t f)"),
             )
 
+        def v_blocks(s, c, t0, t1):
+            for t in range(t0, t1):
+                v_mult(s, c, t, ps_acc, "acc")
+                v_add(s, c, t)
+
+        def v_blocks_ahead(s, c, t0, t1):
+            for t in range(t0, t1):
+                v_mult(s, c, t, ps_y, "y")
+            for t in range(t0, t1):
+                v_add(s, c, t)
+
         st = {}
 
-        def qk_tr(h, s):
-            if s == 0:
-                st[("grp", h)] = grps.tile([P, 2048], BF16, name="grp", tag="grp4", align_bytes=64, bufs=3)
-            bank = ps_prep.tile([P, 512], F32, name="bank_qk", tag="prep")
-            words = raw_w[(s, h // 4)][:, h % 4, :].bitcast(F32)
-            for gu in range(4):
-                nc.tensor.transpose(bank[:, gu * P : (gu + 1) * P], words[:, gu * P : (gu + 1) * P], ident[:])
-            st[("bank", h, s)] = bank
+        def qk_turn(h):
+            st[("grp", h)] = grps.tile([P, 2048], BF16, name="grp", tag="grp4", align_bytes=64, bufs=3)
+            for s in range(2):
+                st[("bank", h, s)] = turn(ps_prep, "prep", raw_w[(s, h // 4)][:, h % 4, :])
 
-        def qk_exit(h, s, on_vector):
+        def qk_leave(h):
             grp_v = st[("grp", h)][:].bitcast(F32).rearrange("p (s g n u) -> p s g n u", s=2, g=2, u=2)
-            src = st[("bank", h, s)][:].rearrange("p (g u n) -> p g n u", g=2, u=2)
-            if on_vector:
-                nc.vector.tensor_copy(out=grp_v[:, s, :, :, :], in_=src)
-            else:
-                nc.scalar.copy(out=grp_v[:, s, :, :, :], in_=src)
+            for s in range(2):
+                leave(st[("bank", h, s)], grp_v[:, s, :, :, :])
 
         def qk_quant(h):
             wc = cods.tile([P, 512], U32, name="wc", align_bytes=64)
@@ -283,12 +262,10 @@ def tile_fluxjointattention_pa_kernel(
             quant(wc, ws, st[("grp", h)], 0, 512, 0)
             st[("codes", h)] = (wc, ws)
 
-        PARTS = (((0, 512, 0, 0),), ((0, 256, 0, 1024), (256, 256, 1, 1536)))
-
         def qk_mult(h, bank):
             wc, ws = st[("codes", h)]
             acc = ps_acc.tile([P, 512], F32, name="acc", tag="acc")
-            for c0, n, s, xw in PARTS[bank]:
+            for c0, n, s, xw in BANK_PARTS[bank]:
                 for g in range(2):
                     wo = (2 * s + g) * P
                     xo = xw + g * n
@@ -306,7 +283,7 @@ def tile_fluxjointattention_pa_kernel(
         def qk_bias(h, bank):
             acc = st[("acc", h, bank)]
             yt = work.tile([P, 512], F32, name="yt")
-            for c0, n, s, xw in PARTS[bank]:
+            for c0, n, s, xw in BANK_PARTS[bank]:
                 nc.scalar.activation(
                     out=yt[:, c0 : c0 + n],
                     in_=acc[:, c0 : c0 + n],
@@ -319,16 +296,15 @@ def tile_fluxjointattention_pa_kernel(
         def qk_back(h, bank):
             yt = st[("yt", h, bank)]
             y = ps_y.tile([P, 512], F32, name="y", tag="y")
-            for b in range(4):
-                if b < BACK_MM:
-                    nc.tensor.matmul(
-                        out=y[:, b * P : (b + 1) * P], lhsT=yt[:, b * P : (b + 1) * P], rhs=ident[:], start=True, stop=True
-                    )
-                else:
-                    nc.tensor.transpose(y[:, b * P : (b + 1) * P], yt[:, b * P : (b + 1) * P], ident[:])
+            for b in range(2):
+                nc.tensor.matmul(
+                    out=y[:, b * P : (b + 1) * P], lhsT=yt[:, b * P : (b + 1) * P], rhs=ident[:], start=True, stop=True
+                )
+            for b in range(2, 4):
+                nc.tensor.transpose(y[:, b * P : (b + 1) * P], yt[:, b * P : (b + 1) * P], ident[:])
             st[("y", h, bank)] = y
 
-        junk = const.tile([P, 8, P], BF16, name="junk")
+        unused = const.tile([P, 8, P], BF16, name="unused")
 
         def qk_square(h, bank):
             if bank == 0:
@@ -337,7 +313,9 @@ def tile_fluxjointattention_pa_kernel(
             for b in range(4):
                 blk = 4 * bank + b
                 nc.scalar.activation(
-                    out=junk[:, blk, :], in_=y[:, b * P : (b + 1) * P], func=ACT.Square,
+                    out=unused[:, blk, :],
+                    in_=y[:, b * P : (b + 1) * P],
+                    func=ACT.Square,
                     accum_out=st[("ss", h)][:, blk : blk + 1],
                 )
 
@@ -354,7 +332,6 @@ def tile_fluxjointattention_pa_kernel(
         def qk_rope(h, bank):
             y = st[("y", h, bank)]
             rs = st[("rs", h)]
-            kind = h // 8
             mw = work.tile([P, 4, 2, P], F32, name="mw")
             for b in range(4):
                 blk = 4 * bank + b
@@ -362,7 +339,7 @@ def tile_fluxjointattention_pa_kernel(
                     out=mw[:, b, :, :],
                     in0=y[:, b * P : (b + 1) * P].unsqueeze(1).to_broadcast([P, 2, P]),
                     scalar=rs[:, blk : blk + 1],
-                    in1=tab[kind][:, blk, :, :],
+                    in1=tab[h // 8][:, blk, :, :],
                     op0=ALU.mult,
                     op1=ALU.mult,
                 )
@@ -393,129 +370,108 @@ def tile_fluxjointattention_pa_kernel(
 
         load_x(0)
         load_x(1)
-        load_v(0, 0, 0, 2)
-        load_v(0, 0, 2, 4)
+        load_w(0, 4, 0, 2)
+        load_w(0, 4, 2, 4)
         load_x(2)
         load_x(3)
-        load_v(0, 1, 0, 2)
-        load_v(0, 1, 2, 4)
+        load_w(0, 5, 0, 2)
+        load_w(0, 5, 2, 4)
         for j in range(2):
             for s in range(2):
                 load_w(s, 0, j, j + 1)
         for s in range(2):
             load_w(s, 0, 2, 4)
-        tables(0)
-
-        def v_back(s, c, t0, t1):
-            for t in range(t0, t1):
-                v_mult(s, c, t, False)
-                v_add(s, c, t)
-
-        def v_wide(s, c, t0, t1):
-            for t in range(t0, t1):
-                v_mult(s, c, t, True)
-            for t in range(t0, t1):
-                v_add(s, c, t)
-
-        def front(h, on_vector):
-            for s in range(2):
-                qk_tr(h, s)
-            qk_exit(h, 0, False)
-            qk_exit(h, 1, on_vector)
 
         for blk in range(4):
-            x_tr(blk)
-            x_exit(blk, False)
+            x_prep(blk)
         x_quant(0)
         v_open(0, 0)
         for j in range(4):
-            v_tr(0, 0, j, j < 2)
-            v_exit(0, 0, j, False)
+            if j < 2:
+                v_prep(0, 0, j, ps_y, "y")
+            else:
+                v_prep(0, 0, j, ps_prep, "prep")
         v_quant(0, 0)
         for blk in range(4, 8):
-            x_tr(blk)
-            x_exit(blk, False)
+            x_prep(blk)
         x_quant(1)
         x_quant(2)
         for s in range(2):
             load_w(s, 1, 0, 4)
-        v_wide(0, 0, 0, 2)
+        v_blocks(0, 0, 0, 2)
+        tables(0)
+        bias_columns()
         v_open(0, 1)
         for j in range(4):
-            v_tr(0, 1, j, False)
-            v_exit(0, 1, j, False)
-        load_v(1, 0, 0, 4)
-        v_wide(0, 0, 2, 6)
-        v_store(0, 0)
-        v_quant(0, 1)
-        load_v(1, 1, 0, 4)
-        bias_columns()
-        front(0, False)
-        front(1, False)
-        for t in range(3):
-            v_mult(0, 1, t, True)
+            v_prep(0, 1, j, ps_y, "y")
+        load_w(1, 4, 0, 4)
+        qk_turn(0)
+        qk_leave(0)
         qk_quant(0)
-        for t in range(3):
-            v_add(0, 1, t)
+        v_blocks_ahead(0, 0, 2, 4)
+        tables(1)
+        qk_turn(1)
+        qk_leave(1)
         qk_mult(0, 0)
         qk_mult(0, 1)
         qk_bias(0, 0)
         qk_bias(0, 1)
-        for t in range(3, 6):
-            v_mult(0, 1, t, True)
         qk_quant(1)
-        for t in range(3, 6):
-            v_add(0, 1, t)
-        v_store(0, 1)
-        front(2, False)
-        tables(1)
-        for h in range(1, NQK + 1):
+        v_blocks_ahead(0, 0, 4, 6)
+        v_store(0, 0)
+        v_quant(0, 1)
+        load_w(1, 5, 0, 4)
+        qk_turn(2)
+        qk_leave(2)
+
+        for h in range(1, HEADS + 1):
             qk_back(h - 1, 0)
             qk_back(h - 1, 1)
-            if h < NQK:
+            if h < HEADS:
                 qk_mult(h, 0)
-            if h + 2 < NQK:
-                qk_tr(h + 2, 0)
-                qk_tr(h + 2, 1)
-            elif h < NQK:
-                if h == NQK - 2:
+            if h + 2 < HEADS:
+                qk_turn(h + 2)
+            elif h < HEADS:
+                if h + 2 == HEADS:
                     v_open(1, 0)
                 for j in range(2):
-                    v_tr(1, 0, 2 * (h + 2 - NQK) + j, False)
-            if h < NQK:
+                    v_turn(1, 0, 2 * (h + 2 - HEADS) + j, ps_prep, "prep")
+            if h < HEADS:
                 qk_mult(h, 1)
             qk_square(h - 1, 0)
             qk_square(h - 1, 1)
-            if h < NQK:
+            if h < HEADS:
                 qk_bias(h, 0)
             qk_sqrt(h - 1)
-            if h < NQK:
+            if h < HEADS:
                 qk_bias(h, 1)
-            if h + 2 < NQK:
-                qk_exit(h + 2, 0, False)
-                qk_exit(h + 2, 1, h in V_EXITS)
-            elif h < NQK:
+            if h + 2 < HEADS:
+                qk_leave(h + 2)
+            elif h < HEADS:
                 for j in range(2):
-                    v_exit(1, 0, 2 * (h + 2 - NQK) + j, False)
+                    v_leave(1, 0, 2 * (h + 2 - HEADS) + j)
             else:
                 v_open(1, 1)
                 for j in range(4):
-                    v_tr(1, 1, j, False)
-                    v_exit(1, 1, j, False)
+                    v_prep(1, 1, j, ps_prep, "prep")
             qk_recip(h - 1)
-            if h + 1 < NQK:
+            if h + 1 < HEADS:
                 qk_quant(h + 1)
-            elif h == NQK:
+            elif h == HEADS:
                 v_quant(1, 0)
-            for bank in range(2):
-                qk_rope(h - 1, bank)
-            for bank in range(2):
-                qk_add(h - 1, bank)
+            if h <= 3:
+                v_blocks(0, 1, 2 * h - 2, 2 * h)
+            if h == 3:
+                v_store(0, 1)
+            qk_rope(h - 1, 0)
+            qk_rope(h - 1, 1)
+            qk_add(h - 1, 0)
+            qk_add(h - 1, 1)
             qk_store(h - 1)
             if h in (1, 5):
                 for s in range(2):
                     load_w(s, (h + 7) // 4, 0, 4)
         v_quant(1, 1)
         for c in range(2):
-            v_back(1, c, 0, 2)
+            v_blocks(1, c, 0, 2)
             v_store(1, c)

@@ -74,7 +74,7 @@ def tile_fluxjointattention_pa_kernel(
         eps_t = const.tile([P, 1], F32, name="eps_t")
         nc.vector.memset(eps_t[:], EPS)
         warm = const.tile([P, 1], F32, name="warm")
-        nc.scalar.activation(out=warm[:], in_=eps_t[:], func=ACT.Sqrt)
+        nc.scalar.activation(out=warm[:], in_=eps_t[:], func=ACT.Abs_reciprocal_sqrt)
         brow = const.tile([P, P], BF16, name="brow")
         nc.vector.memset(brow[:], 0.0)
         ident = const.tile([P, P], F32, name="ident")
@@ -319,14 +319,11 @@ def tile_fluxjointattention_pa_kernel(
                     accum_out=st[("ss", h)][:, blk : blk + 1],
                 )
 
-        def qk_sqrt(h):
-            sd = work.tile([P, 8], F32, name="sd")
-            nc.scalar.activation(out=sd[:], in_=st[("ss", h)][:], func=ACT.Sqrt, bias=eps_t[:], scale=1.0 / P)
-            st[("sd", h)] = sd
-
-        def qk_recip(h):
+        def qk_rms(h):
             rs = work.tile([P, 8], F32, name="rs")
-            nc.vector.reciprocal(out=rs[:], in_=st[("sd", h)][:])
+            nc.scalar.activation(
+                out=rs[:], in_=st[("ss", h)][:], func=ACT.Abs_reciprocal_sqrt, bias=eps_t[:], scale=1.0 / P
+            )
             st[("rs", h)] = rs
 
         def qk_rope(h, bank):
@@ -429,6 +426,7 @@ def tile_fluxjointattention_pa_kernel(
             qk_back(h - 1, 1)
             if h < HEADS:
                 qk_mult(h, 0)
+                qk_mult(h, 1)
             if h + 2 < HEADS:
                 qk_turn(h + 2)
             elif h < HEADS:
@@ -436,13 +434,11 @@ def tile_fluxjointattention_pa_kernel(
                     v_open(1, 0)
                 for j in range(2):
                     v_turn(1, 0, 2 * (h + 2 - HEADS) + j, ps_prep, "prep")
-            if h < HEADS:
-                qk_mult(h, 1)
             qk_square(h - 1, 0)
             qk_square(h - 1, 1)
             if h < HEADS:
                 qk_bias(h, 0)
-            qk_sqrt(h - 1)
+            qk_rms(h - 1)
             if h < HEADS:
                 qk_bias(h, 1)
             if h + 2 < HEADS:
@@ -454,16 +450,15 @@ def tile_fluxjointattention_pa_kernel(
                 v_open(1, 1)
                 for j in range(4):
                     v_prep(1, 1, j, ps_prep, "prep")
-            qk_recip(h - 1)
             if h + 1 < HEADS:
                 qk_quant(h + 1)
             elif h == HEADS:
                 v_quant(1, 0)
+            qk_rope(h - 1, 0)
             if h <= 3:
                 v_blocks(0, 1, 2 * h - 2, 2 * h)
             if h == 3:
                 v_store(0, 1)
-            qk_rope(h - 1, 0)
             qk_rope(h - 1, 1)
             qk_add(h - 1, 0)
             qk_add(h - 1, 1)
@@ -473,5 +468,5 @@ def tile_fluxjointattention_pa_kernel(
                     load_w(s, (h + 7) // 4, 0, 4)
         v_quant(1, 1)
         for c in range(2):
-            v_blocks(1, c, 0, 2)
+            v_blocks_ahead(1, c, 0, 2)
             v_store(1, c)

from contextlib import ExitStack

import concourse.mybir as mybir
from concourse.masks import make_identity

FLOPS = 2 * 1024 * 1024 * 3072

F32 = mybir.dt.float32
BF16 = mybir.dt.bfloat16
U32 = mybir.dt.uint32
U8 = mybir.dt.uint8
FP8X4 = mybir.dt.float8_e4m3fn_x4
ACT = mybir.ActivationFunctionType
ALU = mybir.AluOpType

P = 128
K = 1024
HEADS = 16
EPS = 1e-6
TOKEN_BLOCKS = (6, 2)
FIRST_BLOCK = (0, 6)
BANK_PARTS = (((0, 512, 0, 0),), ((0, 256, 0, 1024), (256, 256, 1, 1536)))


def x_word(blk, g):
    if blk < 4:
        return g * 512 + blk * P
    if blk < 6:
        return 1024 + g * 256 + (blk - 4) * P
    return 1536 + g * 256 + (blk - 6) * P


def tile_fluxjointattention_pa_kernel(
    tc,
    hidden_states_a,
    hidden_states_b,
    image_rotary_emb,
    a_qkv_w,
    a_qkv_b,
    b_qkv_w,
    b_qkv_b,
    norm_q_a_w,
    norm_k_a_w,
    norm_q_b_w,
    norm_k_b_w,
    out_0,
    out_1,
    out_2,
):
    nc = tc.nc
    with ExitStack() as ctx:
        ctx.enter_context(tc.manual_schedule())
        const = ctx.enter_context(tc.tile_pool(name="const", bufs=1))
        raws = ctx.enter_context(tc.tile_pool(name="raws", bufs=4))
        grps = ctx.enter_context(tc.tile_pool(name="grps", bufs=3))
        cods = ctx.enter_context(tc.tile_pool(name="cods", bufs=4))
        work = ctx.enter_context(tc.tile_pool(name="work", bufs=4))
        outs = ctx.enter_context(tc.tile_pool(name="outs", bufs=2))
        ps_prep = ctx.enter_context(tc.psum_pool(name="psprep", bufs=2))
        ps_acc = ctx.enter_context(tc.psum_pool(name="psacc", bufs=2))
        ps_y = ctx.enter_context(tc.psum_pool(name="psy", bufs=4))

        xa_v = hidden_states_a.rearrange("o (p t) k -> p (o t) k", t=6)
        xb_v = hidden_states_b.rearrange("o (p t) k -> p (o t) k", t=2)
        w_v = [
            a_qkv_w.rearrange("(n p) k -> p n k", p=P),
            b_qkv_w.rearrange("(n p) k -> p n k", p=P),
        ]
        rope_v = image_rotary_emb.rearrange("a b s j i c -> (a b s) (j i c)")
        biases = [a_qkv_b, b_qkv_b]
        gains = [norm_q_a_w, norm_k_a_w, norm_q_b_w, norm_k_b_w]
        qk_out = [out_0, out_1]

        eps_t = const.tile([P, 1], F32, name="eps_t")
        nc.vector.memset(eps_t[:], EPS)
        warm = const.tile([P, 1], F32, name="warm")
        nc.scalar.activation(out=warm[:], in_=eps_t[:], func=ACT.Abs_reciprocal_sqrt)
        brow = const.tile([P, P], BF16, name="brow")
        nc.vector.memset(brow[:], 0.0)
        ident = const.tile([P, P], F32, name="ident")
        make_identity(nc, ident[:])

        vbias = const.tile([P, 2, 1024], BF16, name="vbias")
        rope = const.tile([P, 8, 256], BF16, name="rope")
        gain = const.tile([P, 4, P], BF16, name="gain")
        for s in range(2):
            nc.gpsimd.dma_start(
                out=brow[16 * s : 16 * s + 16, :],
                in_=biases[s][0:2048].rearrange("(r f) -> r f", f=P),
            )
        nc.gpsimd.dma_start(out=vbias[:, 0, :], in_=biases[0][2048:3072].partition_broadcast(P))
        nc.gpsimd.dma_start(out=rope[:, 0:6, :], in_=rope_v[256:1024, :].rearrange("(p t) e -> p t e", t=6))
        nc.gpsimd.dma_start(out=rope[:, 6:8, :], in_=rope_v[0:256, :].rearrange("(p t) e -> p t e", t=2))
        for m in (0, 2, 1, 3):
            nc.gpsimd.dma_start(out=gain[:, m, :], in_=gains[m].partition_broadcast(P))
        nc.gpsimd.dma_start(out=vbias[:, 1, :], in_=biases[1][2048:3072].partition_broadcast(P))

        def turn(pool, tag, rows):
            bank = pool.tile([P, 512], F32, name="bank_" + tag, tag=tag)
            words = rows.bitcast(F32)
            for gu in range(4):
                nc.tensor.transpose(bank[:, gu * P : (gu + 1) * P], words[:, gu * P : (gu + 1) * P], ident[:])
            return bank

        def leave(bank, dst):
            nc.scalar.copy(out=dst, in_=bank[:].rearrange("p (g u n) -> p g n u", g=2, u=2))

        def quant(codes, scales, grp, w0, w1, g0):
            nc.vector.quantize_mx(
                out=codes[:, w0:w1].bitcast(FP8X4),
                scales=scales[:, w0:w1],
                in_=grp[:, g0 : g0 + 4 * (w1 - w0)],
            )

        raw_w = {}

        def load_w(s, chunk, j0, j1):
            if j0 == 0:
                if chunk < 4:
                    raw_w[(s, chunk)] = raws.tile([P, 4, K], BF16, name="raw_w%d_%d" % (s, chunk), tag="raw")
                else:
                    raw_w[(s, chunk)] = raws.tile([P, 4, K], BF16, name="raw_w%d_%d" % (s, chunk), tag="rawv", bufs=2)
            nc.sync.dma_start(out=raw_w[(s, chunk)][:, j0:j1, :], in_=w_v[s][:, 4 * chunk + j0 : 4 * chunk + j1, :])

        raw_x = [raws.tile([P, 4, K], BF16, name="raw_x%d" % i, tag="raw") for i in range(2)]
        x_codes = const.tile([P, 2048], U32, name="x_codes", align_bytes=64)
        x_scale = const.tile([P, 2048], U8, name="x_scale", align_bytes=64)
        xg = [grps.tile([P, 4096], BF16, name="xg%d" % i, tag="grp8", align_bytes=64) for i in range(2)]
        xg0_v = xg[0][:].bitcast(F32).rearrange("p (g n u) -> p g n u", g=2, u=2)
        xg1_v = xg[1][:].bitcast(F32).rearrange("p (c g n u) -> p c g n u", c=2, g=2, u=2)

        def load_x(pair):
            src = (xa_v[:, 0:2, :], xa_v[:, 2:4, :], xa_v[:, 4:6, :], xb_v)[pair]
            nc.sync.dma_start(out=raw_x[pair // 2][:, 2 * (pair % 2) : 2 * (pair % 2) + 2, :], in_=src)

        def x_prep(blk):
            pool, tag = ((ps_prep, "prep"), (ps_y, "y"), (ps_y, "y"), (ps_prep, "prep"))[blk // 2]
            bank = turn(pool, tag, raw_x[blk // 4][:, blk % 4, :])
            if blk < 4:
                leave(bank, xg0_v[:, :, blk * P : (blk + 1) * P, :])
            else:
                c, tb = divmod(blk - 4, 2)
                leave(bank, xg1_v[:, c, :, tb * P : (tb + 1) * P, :])

        def x_quant(c):
            if c == 0:
                quant(x_codes, x_scale, xg[0], 0, 1024, 0)
            else:
                quant(x_codes, x_scale, xg[1], 512 + 512 * c, 1024 + 512 * c, 2048 * (c - 1))

        bias_t = const.tile([P, 32], F32, name="bias_t")

        def bias_columns():
            brow_f = const.tile([P, P], F32, name="brow_f")
            nc.scalar.copy(out=brow_f[:], in_=brow[:])
            bias_ps = ps_prep.tile([P, 512], F32, name="bias_ps", tag="prep")
            nc.tensor.transpose(bias_ps[:, 0:P], brow_f[:], ident[:])
            nc.scalar.copy(out=bias_t[:], in_=bias_ps[:, 0:32])

        gain_p = gain[:].rearrange("p m (j c) -> p m j c", c=2)
        tab = [const.tile([P, 8, 2, P], F32, name="tab%d" % kind) for kind in range(2)]
        rope_q = rope[:].rearrange("p t (j q) -> p t j q", q=4)

        def tables(kind):
            for s in range(2):
                b0 = FIRST_BLOCK[s]
                b1 = b0 + TOKEN_BLOCKS[s]
                g_bc = gain_p[:, 2 * s + kind, :, :].unsqueeze(1).to_broadcast([P, b1 - b0, 64, 2])
                nc.vector.tensor_tensor(
                    out=tab[kind][:, b0:b1, 0, :].rearrange("p t (j c) -> p t j c", c=2),
                    in0=rope_q[:, b0:b1, :, 0:4:3],
                    in1=g_bc,
                    op=ALU.mult,
                )
                nc.vector.tensor_tensor(
                    out=tab[kind][:, b0:b1, 1, :].rearrange("p t (j c) -> p t j c", c=2),
                    in0=rope_q[:, b0:b1, :, 2:0:-1],
                    in1=g_bc,
                    op=ALU.mult,
                )

        vst = {}

        def v_open(s, c):
            vst[("grp", s, c)] = grps.tile([P, 4096], BF16, name="vg", tag="grp8", align_bytes=64)

        def v_turn(s, c, j, pool, tag):
            vst[("bank", s, c, j)] = turn(pool, tag, raw_w[(s, 4 + c)][:, j, :])

        def v_leave(s, c, j):
            vg_v = vst[("grp", s, c)][:].bitcast(F32).rearrange("p (g n u) -> p g n u", g=2, u=2)
            leave(vst[("bank", s, c, j)], vg_v[:, :, j * P : (j + 1) * P, :])

        def v_prep(s, c, j, pool, tag):
            v_turn(s, c, j, pool, tag)
            v_leave(s, c, j)

        def v_quant(s, c):
            vc = const.tile([P, 1024], U32, name="vc%d%d" % (s, c), align_bytes=64)
            vs = const.tile([P, 1024], U8, name="vs%d%d" % (s, c), align_bytes=64)
            quant(vc, vs, vst[("grp", s, c)], 0, 1024, 0)
            vst[("codes", s, c)] = (vc, vs)
            vst[("out", s, c)] = outs.tile([P, 4, TOKEN_BLOCKS[s], P], F32, name="ov%d" % s)

        def v_mult(s, c, t, pool, tag):
            vc, vs = vst[("codes", s, c)]
            acc = pool.tile([P, 512], F32, name="vacc", tag=tag)
            for g in range(2):
                xo = x_word(FIRST_BLOCK[s] + t, g)
                nc.tensor.matmul_mx(
                    out=acc[:],
                    lhsT=x_codes[:, xo : xo + P].bitcast(FP8X4),
                    lhsT_scale=x_scale[:, xo : xo + P],
                    rhs=vc[:, g * 512 : (g + 1) * 512].bitcast(FP8X4),
                    rhs_scale=vs[:, g * 512 : (g + 1) * 512],
                    start=(g == 0),
                    stop=(g == 1),
                )
            vst[("acc", s, c, t)] = acc

        def v_add(s, c, t):
            nc.vector.tensor_tensor(
                out=vst[("out", s, c)][:, :, t, :],
                in0=vst[("acc", s, c, t)][:].rearrange("p (h f) -> p h f", h=4),
                in1=vbias[:, s, c * 512 : (c + 1) * 512].rearrange("p (h f) -> p h f", h=4),
                op=ALU.add,
            )

        def v_store(s, c):
            lo, hi = ((256, 1024), (0, 256))[s]
            nc.sync.dma_start(
                out=out_2[0, 4 * c : 4 * c + 4, lo:hi, :].rearrange("h (p t) f -> p h (t f)", t=TOKEN_BLOCKS[s]),
                in_=vst[("out", s, c)][:].rearrange("p h t f -> p h (t f)"),
            )

        def v_blocks(s, c, t0, t1):
            for t in range(t0, t1):
                v_mult(s, c, t, ps_acc, "acc")
                v_add(s, c, t)

        def v_blocks_ahead(s, c, t0, t1):
            for t in range(t0, t1):
                v_mult(s, c, t, ps_y, "y")
            for t in range(t0, t1):
                v_add(s, c, t)

        st = {}

        def qk_turn(h):
            st[("grp", h)] = grps.tile([P, 2048], BF16, name="grp", tag="grp4", align_bytes=64, bufs=3)
            for s in range(2):
                st[("bank", h, s)] = turn(ps_prep, "prep", raw_w[(s, h // 4)][:, h % 4, :])

        def qk_leave(h):
            grp_v = st[("grp", h)][:].bitcast(F32).rearrange("p (s g n u) -> p s g n u", s=2, g=2, u=2)
            for s in range(2):
                leave(st[("bank", h, s)], grp_v[:, s, :, :, :])

        def qk_quant(h):
            wc = cods.tile([P, 512], U32, name="wc", align_bytes=64)
            ws = cods.tile([P, 512], U8, name="ws", align_bytes=64)
            quant(wc, ws, st[("grp", h)], 0, 512, 0)
            st[("codes", h)] = (wc, ws)

        def qk_mult(h, bank):
            wc, ws = st[("codes", h)]
            acc = ps_acc.tile([P, 512], F32, name="acc", tag="acc")
            for c0, n, s, xw in BANK_PARTS[bank]:
                for g in range(2):
                    wo = (2 * s + g) * P
                    xo = xw + g * n
                    nc.tensor.matmul_mx(
                        out=acc[:, c0 : c0 + n],
                        lhsT=wc[:, wo : wo + P].bitcast(FP8X4),
                        lhsT_scale=ws[:, wo : wo + P],
                        rhs=x_codes[:, xo : xo + n].bitcast(FP8X4),
                        rhs_scale=x_scale[:, xo : xo + n],
                        start=(g == 0),
                        stop=(g == 1),
                    )
            st[("acc", h, bank)] = acc

        def qk_bias(h, bank):
            acc = st[("acc", h, bank)]
            yt = work.tile([P, 512], F32, name="yt")
            for c0, n, s, xw in BANK_PARTS[bank]:
                nc.scalar.activation(
                    out=yt[:, c0 : c0 + n],
                    in_=acc[:, c0 : c0 + n],
                    func=ACT.Identity,
                    bias=bias_t[:, 16 * s + h : 16 * s + h + 1],
                    scale=1.0,
                )
            st[("yt", h, bank)] = yt

        def qk_back(h, bank):
            yt = st[("yt", h, bank)]
            y = ps_y.tile([P, 512], F32, name="y", tag="y")
            for b in range(2):
                nc.tensor.matmul(
                    out=y[:, b * P : (b + 1) * P], lhsT=yt[:, b * P : (b + 1) * P], rhs=ident[:], start=True, stop=True
                )
            for b in range(2, 4):
                nc.tensor.transpose(y[:, b * P : (b + 1) * P], yt[:, b * P : (b + 1) * P], ident[:])
            st[("y", h, bank)] = y

        unused = const.tile([P, 8, P], BF16, name="unused")

        def qk_square(h, bank):
            if bank == 0:
                st[("ss", h)] = work.tile([P, 8], F32, name="ss")
            y = st[("y", h, bank)]
            for b in range(4):
                blk = 4 * bank + b
                nc.scalar.activation(
                    out=unused[:, blk, :],
                    in_=y[:, b * P : (b + 1) * P],
                    func=ACT.Square,
                    accum_out=st[("ss", h)][:, blk : blk + 1],
                )

        def qk_rms(h):
            rs = work.tile([P, 8], F32, name="rs")
            nc.scalar.activation(
                out=rs[:], in_=st[("ss", h)][:], func=ACT.Abs_reciprocal_sqrt, bias=eps_t[:], scale=1.0 / P
            )
            st[("rs", h)] = rs

        def qk_rope(h, bank):
            y = st[("y", h, bank)]
            rs = st[("rs", h)]
            mw = work.tile([P, 4, 2, P], F32, name="mw")
            for b in range(4):
                blk = 4 * bank + b
                nc.vector.scalar_tensor_tensor(
                    out=mw[:, b, :, :],
                    in0=y[:, b * P : (b + 1) * P].unsqueeze(1).to_broadcast([P, 2, P]),
                    scalar=rs[:, blk : blk + 1],
                    in1=tab[h // 8][:, blk, :, :],
                    op0=ALU.mult,
                    op1=ALU.mult,
                )
            st[("m", h, bank)] = mw

        def qk_add(h, bank):
            if bank == 0:
                st[("o", h)] = outs.tile([P, 8, P], F32, name="o", bufs=3)
            mw = st[("m", h, bank)]
            nc.vector.tensor_tensor(
                out=st[("o", h)][:, 4 * bank : 4 * bank + 4, :].rearrange("p b (j c) -> p b j c", c=2),
                in0=mw[:, :, 0, :].rearrange("p b (j c) -> p b j c", c=2),
                in1=mw[:, :, 1, :].rearrange("p b (j c) -> p b j c", c=2)[:, :, :, ::-1],
                op=ALU.add,
            )

        def qk_store(h):
            dst = qk_out[h // 8]
            o = st[("o", h)]
            nc.sync.dma_start(
                out=dst[0, h % 8, 256:1024, :].rearrange("(p t) f -> p (t f)", t=6),
                in_=o[:, 0:6, :].rearrange("p t f -> p (t f)"),
            )
            nc.sync.dma_start(
                out=dst[0, h % 8, 0:256, :].rearrange("(p t) f -> p (t f)", t=2),
                in_=o[:, 6:8, :].rearrange("p t f -> p (t f)"),
            )

        load_x(0)
        load_x(1)
        load_w(0, 4, 0, 2)
        load_w(0, 4, 2, 4)
        load_x(2)
        load_x(3)
        load_w(0, 5, 0, 2)
        load_w(0, 5, 2, 4)
        for j in range(2):
            for s in range(2):
                load_w(s, 0, j, j + 1)
        for s in range(2):
            load_w(s, 0, 2, 4)

        for blk in range(4):
            x_prep(blk)
        x_quant(0)
        v_open(0, 0)
        for j in range(4):
            if j < 2:
                v_prep(0, 0, j, ps_y, "y")
            else:
                v_prep(0, 0, j, ps_prep, "prep")
        v_quant(0, 0)
        for blk in range(4, 8):
            x_prep(blk)
        x_quant(1)
        x_quant(2)
        for s in range(2):
            load_w(s, 1, 0, 4)
        v_blocks(0, 0, 0, 2)
        tables(0)
        bias_columns()
        v_open(0, 1)
        for j in range(4):
            v_prep(0, 1, j, ps_y, "y")
        load_w(1, 4, 0, 4)
        qk_turn(0)
        qk_leave(0)
        qk_quant(0)
        v_blocks_ahead(0, 0, 2, 4)
        tables(1)
        qk_turn(1)
        qk_leave(1)
        qk_mult(0, 0)
        qk_mult(0, 1)
        qk_bias(0, 0)
        qk_bias(0, 1)
        qk_quant(1)
        v_blocks_ahead(0, 0, 4, 6)
        v_store(0, 0)
        v_quant(0, 1)
        load_w(1, 5, 0, 4)
        qk_turn(2)
        qk_leave(2)

        for h in range(1, HEADS + 1):
            qk_back(h - 1, 0)
            qk_back(h - 1, 1)
            if h < HEADS:
                qk_mult(h, 0)
                qk_mult(h, 1)
            if h + 2 < HEADS:
                qk_turn(h + 2)
            elif h < HEADS:
                if h + 2 == HEADS:
                    v_open(1, 0)
                for j in range(2):
                    v_turn(1, 0, 2 * (h + 2 - HEADS) + j, ps_prep, "prep")
            qk_square(h - 1, 0)
            qk_square(h - 1, 1)
            if h < HEADS:
                qk_bias(h, 0)
            qk_rms(h - 1)
            if h < HEADS:
                qk_bias(h, 1)
            if h + 2 < HEADS:
                qk_leave(h + 2)
            elif h < HEADS:
                for j in range(2):
                    v_leave(1, 0, 2 * (h + 2 - HEADS) + j)
            else:
                v_open(1, 1)
                for j in range(4):
                    v_prep(1, 1, j, ps_prep, "prep")
            if h + 1 < HEADS:
                qk_quant(h + 1)
            elif h == HEADS:
                v_quant(1, 0)
            qk_rope(h - 1, 0)
            if h <= 3:
                v_blocks(0, 1, 2 * h - 2, 2 * h)
            if h == 3:
                v_store(0, 1)
            qk_rope(h - 1, 1)
            qk_add(h - 1, 0)
            qk_add(h - 1, 1)
            qk_store(h - 1)
            if h in (1, 5):
                for s in range(2):
                    load_w(s, (h + 7) // 4, 0, 4)
        v_quant(1, 1)
        for c in range(2):
            v_blocks_ahead(1, c, 0, 2)
            v_store(1, c)
